import numpy as np
import ml_dtypes


def mxq(x, axis, fmt="e4m3"):
    dtype, down = {"e4m3": (ml_dtypes.float8_e4m3fn, 7), "e5m2": (ml_dtypes.float8_e5m2, 14)}[fmt]
    v = np.moveaxis(np.asarray(x, np.float32).astype(ml_dtypes.bfloat16).astype(np.float64), axis, -1)
    blocks = v.reshape(v.shape[:-1] + (-1, 32))
    amax = np.abs(blocks).max(-1, keepdims=True)
    byte = np.maximum(np.where(amax > 0, np.frexp(amax)[1] - 1 + 127, 0) - down, 1)
    scale = np.exp2(byte - 127.0)
    codes = (blocks / scale).astype(np.float32).astype(dtype).astype(np.float64)
    return np.moveaxis((codes * scale).reshape(v.shape), -1, axis)


BF16 = ml_dtypes.bfloat16


def bf(x):
    return np.asarray(x, np.float32).astype(BF16)


def f64(x):
    return np.asarray(x).astype(np.float64)


B, TQ, TV, H, DH = 2, 512, 2048, 8, 128
D = H * DH


def setup_inputs():
    return {"query": bf(np.random.standard_normal((B, TQ, D))),
            "k": bf(np.random.standard_normal((B, TV, D))),
            "value": bf(np.random.standard_normal((B, TV, DH)) * 0.5)}


def reference(query, k, value):
    qs = f64(query).reshape(B, TQ, H, DH).transpose(0, 2, 1, 3)
    ks = f64(k).reshape(B, TV, H, DH).transpose(0, 2, 3, 1)
    qk = (qs @ ks) * DH ** -0.5
    e = np.exp(qk - qk.max(axis=1, keepdims=True))
    w = e / e.sum(axis=1, keepdims=True)
    ctx = mxq(w, 3, "e4m3") @ mxq(f64(value), 1, "e4m3")[:, None]
    return ctx.transpose(0, 2, 1, 3).reshape(B, TQ, D)

@@ -1,0 +1,259 @@
+from contextlib import ExitStack
+
+import concourse.mybir as mybir
+from concourse.masks import make_identity
+
+B, TQ, TV, H, DH = 2, 512, 2048, 8, 128
+FLOPS = 2 * 2 * B * H * TQ * TV * DH
+
+F32 = mybir.dt.float32
+BF16 = mybir.dt.bfloat16
+U32 = mybir.dt.uint32
+U8 = mybir.dt.uint8
+FP8X4 = mybir.dt.float8_e4m3fn_x4
+ALU = mybir.AluOpType
+ACT = mybir.ActivationFunctionType
+
+P = 128
+PACK = 4
+K_PASS = P * PACK
+N_PASS = TV // K_PASS
+QT = TQ // P
+QH = 64
+N_BLOCK = B * QT * N_PASS
+SUM_LAG = 2
+HEADS_ON_GPSIMD = 8
+MANUAL = False
+
+
+def tile_multiheadattention_pa_kernel(tc, query, k, value, out):
+    nc = tc.nc
+    with ExitStack() as ctx:
+        if MANUAL:
+            ctx.enter_context(tc.manual_schedule())
+        const = ctx.enter_context(tc.tile_pool(name="const", bufs=1))
+        kraw_pool = ctx.enter_context(tc.tile_pool(name="kraw", bufs=2))
+        qraw_pool = ctx.enter_context(tc.tile_pool(name="qraw", bufs=1))
+        kt_pool = ctx.enter_context(tc.tile_pool(name="kt", bufs=5))
+        qt_pool = ctx.enter_context(tc.tile_pool(name="qt", bufs=2))
+        v_stage = ctx.enter_context(tc.tile_pool(name="vstage", bufs=1))
+        v_keep = ctx.enter_context(tc.tile_pool(name="vkeep", bufs=2))
+        e_pool = ctx.enter_context(tc.tile_pool(name="e", bufs=5))
+        c_pool = ctx.enter_context(tc.tile_pool(name="c", bufs=4))
+        r_pool = ctx.enter_context(tc.tile_pool(name="r", bufs=2))
+        w_pool = ctx.enter_context(tc.tile_pool(name="w", bufs=2))
+        code_pool = ctx.enter_context(tc.tile_pool(name="code", bufs=5))
+        o_pool = ctx.enter_context(tc.tile_pool(name="o", bufs=1))
+        ps_sc = ctx.enter_context(tc.psum_pool(name="ps_sc", bufs=4))
+        ps_sum = ctx.enter_context(tc.psum_pool(name="ps_sum", bufs=2))
+        ps_misc = ctx.enter_context(tc.psum_pool(name="ps_misc", bufs=2))
+
+        ident_bf = const.tile([P, P], BF16)
+        make_identity(nc, ident_bf[:])
+        ident_f = const.tile([P, P], F32)
+        make_identity(nc, ident_f[:])
+
+        kraw, qraw, k_t, q_t = {}, {}, {}, {}
+        v_codes, v_scales = {}, {}
+        e, sum_t, r_t, r_sb, w, codes, scales = {}, {}, {}, {}, {}, {}, {}
+
+        def where(i):
+            return i // (QT * N_PASS), (i // N_PASS) % QT, i % N_PASS
+
+        def load_k(b, g):
+            raw = kraw_pool.tile([P, PACK, H * DH], BF16)
+            nc.sync.dma_start(
+                out=raw[:].rearrange("p j c -> p (j c)"),
+                in_=k[b, g * K_PASS : (g + 1) * K_PASS, :].rearrange("(p j) c -> p (j c)", j=PACK),
+            )
+            kraw[(b, g)] = raw
+
+        def load_q(b):
+            raw = qraw_pool.tile([P, QT, H * DH], BF16)
+            nc.sync.dma_start(out=raw[:], in_=query[b].rearrange("(t p) c -> p t c", p=P))
+            qraw[b] = raw
+
+        def prep_k(b, g, j):
+            if j == 0:
+                kt = kt_pool.tile([P, PACK, H, P], BF16)
+                k_t[(b, g)] = kt
+            tp = ps_misc.tile([P, H, P], BF16, tag="misc")
+            for h in range(H):
+                nc.tensor.transpose(out=tp[:, h, :], in_=kraw[(b, g)][:, j, h * DH : (h + 1) * DH], identity=ident_bf[:])
+            nc.scalar.copy(out=k_t[(b, g)][:, j], in_=tp[:])
+
+        def prep_q(b, t):
+            qt = qt_pool.tile([P, H, P], BF16)
+            tp = ps_misc.tile([P, H, P], BF16, tag="misc")
+            for h in range(H):
+                nc.tensor.transpose(out=tp[:, h, :], in_=qraw[b][:, t, h * DH : (h + 1) * DH], identity=ident_bf[:])
+            nc.scalar.copy(out=qt[:], in_=tp[:])
+            q_t[(b, t)] = qt
+
+        def prep_v(b):
+            raw = v_stage.tile([P, N_PASS, PACK, DH], BF16)
+            nc.sync.dma_start(out=raw[:], in_=value[b].rearrange("(g p j) d -> p g j d", p=P, j=PACK))
+            grouped = v_stage.tile([P, N_PASS, DH, PACK], BF16, align_bytes=64)
+            nc.vector.tensor_copy(out=grouped[:], in_=raw[:].rearrange("p g j d -> p g d j"))
+            vc = v_keep.tile([P, N_PASS * DH], U32, align_bytes=64)
+            vs = v_keep.tile([P, N_PASS * DH], U8, align_bytes=64)
+            nc.vector.quantize_mx(
+                out=vc[:].bitcast(FP8X4), scales=vs[:], in_=grouped[:].rearrange("p g d j -> p (g d j)")
+            )
+            v_codes[b] = vc
+            v_scales[b] = vs
+
+        def scores(i, j):
+            b, t, g = where(i)
+            if j == 0:
+                et = e_pool.tile([P, PACK, H, P], F32)
+                e[i] = et
+            for qh in range(P // QH):
+                cols = slice(qh * QH, (qh + 1) * QH)
+                sc = ps_sc.tile([P, H * QH], F32)
+                for h in range(H):
+                    nc.tensor.matmul(
+                        out=sc[:, h * QH : (h + 1) * QH],
+                        lhsT=k_t[(b, g)][:, j, h, :],
+                        rhs=q_t[(b, t)][:, h, cols],
+                        start=True,
+                        stop=True,
+                    )
+                top = c_pool.tile([P, QH], F32)
+                nc.vector.tensor_reduce(
+                    out=top[:], in_=sc[:].rearrange("p (h q) -> p q h", h=H), axis=mybir.AxisListType.X, op=ALU.max
+                )
+                nc.vector.tensor_tensor(
+                    out=e[i][:, j, :, cols],
+                    in0=sc[:].rearrange("p (h q) -> p h q", h=H),
+                    in1=top[:].unsqueeze(1).to_broadcast([P, H, QH]),
+                    op=ALU.subtract,
+                )
+            flat = e[i][:, j].rearrange("p h q -> p (h q)")
+            nc.scalar.activation(out=flat, in_=flat, func=ACT.Exp, scale=DH**-0.5)
+
+        def head_sum(i, j):
+            if j == 0:
+                st = ps_sum.tile([P, PACK * P], F32)
+                sum_t[i] = st
+            for h in range(H):
+                nc.tensor.matmul(
+                    out=sum_t[i][:, j * P : (j + 1) * P],
+                    lhsT=e[i][:, j, h, :],
+                    rhs=ident_f[:],
+                    is_transpose=True,
+                    start=(h == 0),
+                    stop=(h == H - 1),
+                )
+
+        def log_recip(i):
+            rt = r_pool.tile([P, 2, PACK * P], F32)
+            for n in range(2):
+                nc.scalar.activation(out=rt[:, n], in_=sum_t[i - 1 + n][:], func=ACT.Ln)
+            flat = rt[:].rearrange("p n c -> p (n c)")
+            nc.scalar.activation(out=flat, in_=flat, func=ACT.Exp, scale=-1.0)
+            r_t[i - 1] = rt[:, 0]
+            r_t[i] = rt[:, 1]
+
+        def recip_back(i):
+            rp = ps_misc.tile([P, PACK * P], F32, tag="misc")
+            for j in range(PACK):
+                nc.tensor.transpose(out=rp[:, j * P : (j + 1) * P], in_=r_t[i][:, j * P : (j + 1) * P], identity=ident_f[:])
+            rs = r_pool.tile([P, P, PACK], F32)
+            nc.scalar.copy(out=rs[:], in_=rp[:].rearrange("p (j q) -> p q j", j=PACK))
+            r_sb[i] = rs
+
+        def weights(i):
+            wt = w_pool.tile([P, H, P, PACK], BF16, align_bytes=64)
+            w[i] = wt
+            ev = e[i][:].rearrange("p j h q -> p h q j")
+            for eng, h0, h1 in ((nc.gpsimd, 0, HEADS_ON_GPSIMD), (nc.vector, HEADS_ON_GPSIMD, H)):
+                if h1 > h0:
+                    eng.tensor_tensor(
+                        out=wt[:, h0:h1],
+                        in0=ev[:, h0:h1],
+                        in1=r_sb[i][:].unsqueeze(1).to_broadcast([P, h1 - h0, P, PACK]),
+                        op=ALU.mult,
+                    )
+
+        def quantise(i):
+            cd = code_pool.tile([P, H * P], U32, align_bytes=64)
+            sl = code_pool.tile([P, H * P], U8, align_bytes=64)
+            nc.vector.quantize_mx(
+                out=cd[:].bitcast(FP8X4), scales=sl[:], in_=w[i][:].rearrange("p h q j -> p (h q j)")
+            )
+            codes[i] = cd
+            scales[i] = sl
+
+        def context(b, t):
+            res = o_pool.tile([P, H * DH], F32)
+            per_bank = 4
+            for half in range(H // per_bank):
+                acc = ps_misc.tile([P, per_bank * DH], F32, tag="misc")
+                for hh in range(per_bank):
+                    h = half * per_bank + hh
+                    for g in range(N_PASS):
+                        i = (b * QT + t) * N_PASS + g
+                        nc.tensor.matmul_mx(
+                            out=acc[:, hh * DH : (hh + 1) * DH],
+                            lhsT=codes[i][:, h * P : (h + 1) * P].bitcast(FP8X4),
+                            lhsT_scale=scales[i][:, h * P : (h + 1) * P],
+                            rhs=v_codes[b][:, g * DH : (g + 1) * DH].bitcast(FP8X4),
+                            rhs_scale=v_scales[b][:, g * DH : (g + 1) * DH],
+                            start=(g == 0),
+                            stop=(g == N_PASS - 1),
+                        )
+                nc.scalar.copy(out=res[:, half * per_bank * DH : (half + 1) * per_bank * DH], in_=acc[:])
+            nc.sync.dma_start(out=out[b, t * P : (t + 1) * P, :], in_=res[:])
+
+        extra = {}
+
+        def at(s, fn, *args):
+            extra[s] = extra.get(s, []) + [(fn, args)]
+
+        per_b = QT * N_PASS * PACK
+        for g in range(N_PASS):
+            for j in range(PACK):
+                s_need = g * PACK + j
+                if s_need >= 2:
+                    at(s_need - 2, prep_k, 0, g, j)
+                at(per_b - 16 + g * PACK + j, prep_k, 1, g, j)
+            at(per_b - 20 + g * PACK, load_k, 1, g)
+        for b in range(B):
+            for t in range(QT):
+                if (b, t) != (0, 0):
+                    at(b * per_b + t * 16 - 3, prep_q, b, t)
+        at(per_b - 18, load_q, 1)
+        at(per_b - 14, prep_v, 1)
+
+        load_k(0, 0)
+        load_q(0)
+        load_k(0, 1)
+        prep_q(0, 0)
+        prep_k(0, 0, 0)
+        prep_k(0, 0, 1)
+        prep_v(0)
+        at(2, load_k, 0, 2)
+        at(6, load_k, 0, 3)
+
+        for s in range(N_BLOCK * PACK + 16):
+            i, j = s // PACK, s % PACK
+            if i < N_BLOCK:
+                scores(i, j)
+            s1 = s - 11
+            if s1 >= 0 and s1 % PACK == 0 and s1 // PACK < N_BLOCK:
+                recip_back(s1 // PACK)
+                weights(s1 // PACK)
+            s2 = s - SUM_LAG
+            if 0 <= s2 < N_BLOCK * PACK:
+                head_sum(s2 // PACK, s2 % PACK)
+                if s2 % (2 * PACK) == 2 * PACK - 1:
+                    log_recip(s2 // PACK)
+            s3 = s - 15
+            if s3 >= 0 and s3 % PACK == 0 and s3 // PACK < N_BLOCK:
+                quantise(s3 // PACK)
+                b, t, g = where(s3 // PACK)
+                if g == N_PASS - 1:
+                    context(b, t)
+            for fn, args in extra.get(s, []):
+                fn(*args)

@@ -21,9 +21,16 @@ N_PASS = TV // K_PASS
 QT = TQ // P
 QH = 64
 N_BLOCK = B * QT * N_PASS
-SUM_LAG = 2
-HEADS_ON_GPSIMD = 8
-MANUAL = False
+RUN = 4
+SUM_LAG = 3
+BACK_AT = (14, 16)
+QUANT_AT = (20, 24)
+CONTEXT_LAG = 4
+TAIL_BLOCKS = 4
+TAIL_HEADS_ON_GPSIMD = 3
+VMUL_AT = (18, 22)
+HEADS_ON_GPSIMD = 6
+MANUAL = True
 
 
 def tile_multiheadattention_pa_kernel(tc, query, k, value, out):
@@ -44,8 +51,8 @@ def tile_multiheadattention_pa_kernel(tc, query, k, value, out):
         w_pool = ctx.enter_context(tc.tile_pool(name="w", bufs=2))
         code_pool = ctx.enter_context(tc.tile_pool(name="code", bufs=5))
         o_pool = ctx.enter_context(tc.tile_pool(name="o", bufs=1))
-        ps_sc = ctx.enter_context(tc.psum_pool(name="ps_sc", bufs=4))
-        ps_sum = ctx.enter_context(tc.psum_pool(name="ps_sum", bufs=2))
+        ps_sc = ctx.enter_context(tc.psum_pool(name="ps_sc", bufs=3))
+        ps_sum = ctx.enter_context(tc.psum_pool(name="ps_sum", bufs=3))
         ps_misc = ctx.enter_context(tc.psum_pool(name="ps_misc", bufs=2))
 
         ident_bf = const.tile([P, P], BF16)
@@ -53,25 +60,31 @@ def tile_multiheadattention_pa_kernel(tc, query, k, value, out):
         ident_f = const.tile([P, P], F32)
         make_identity(nc, ident_f[:])
 
-        kraw, qraw, k_t, q_t = {}, {}, {}, {}
+        kraw, qraw, vraw, k_t, q_t = {}, {}, {}, {}, {}
         v_codes, v_scales = {}, {}
         e, sum_t, r_t, r_sb, w, codes, scales = {}, {}, {}, {}, {}, {}, {}
 
         def where(i):
             return i // (QT * N_PASS), (i // N_PASS) % QT, i % N_PASS
 
-        def load_k(b, g):
+        def load_k(b, g, pieces):
             raw = kraw_pool.tile([P, PACK, H * DH], BF16)
-            nc.sync.dma_start(
-                out=raw[:].rearrange("p j c -> p (j c)"),
-                in_=k[b, g * K_PASS : (g + 1) * K_PASS, :].rearrange("(p j) c -> p (j c)", j=PACK),
-            )
+            rows = k[b, g * K_PASS : (g + 1) * K_PASS, :].rearrange("(p j) c -> p j c", j=PACK)
+            step = PACK // pieces
+            for n in range(pieces):
+                nc.sync.dma_start(out=raw[:, n * step : (n + 1) * step, :], in_=rows[:, n * step : (n + 1) * step, :])
             kraw[(b, g)] = raw
 
-        def load_q(b):
-            raw = qraw_pool.tile([P, QT, H * DH], BF16)
-            nc.sync.dma_start(out=raw[:], in_=query[b].rearrange("(t p) c -> p t c", p=P))
-            qraw[b] = raw
+        def load_q(b, t0, t1):
+            if t0 == 0:
+                raw = qraw_pool.tile([P, QT, H * DH], BF16)
+                qraw[b] = raw
+            nc.sync.dma_start(out=qraw[b][:, t0:t1, :], in_=query[b].rearrange("(t p) c -> p t c", p=P)[:, t0:t1, :])
+
+        def load_v(b):
+            raw = v_stage.tile([P, N_PASS, PACK, DH], BF16)
+            nc.sync.dma_start(out=raw[:], in_=value[b].rearrange("(g p j) d -> p g j d", p=P, j=PACK))
+            vraw[b] = raw
 
         def prep_k(b, g, j):
             if j == 0:
@@ -91,10 +104,8 @@ def tile_multiheadattention_pa_kernel(tc, query, k, value, out):
             q_t[(b, t)] = qt
 
         def prep_v(b):
-            raw = v_stage.tile([P, N_PASS, PACK, DH], BF16)
-            nc.sync.dma_start(out=raw[:], in_=value[b].rearrange("(g p j) d -> p g j d", p=P, j=PACK))
             grouped = v_stage.tile([P, N_PASS, DH, PACK], BF16, align_bytes=64)
-            nc.vector.tensor_copy(out=grouped[:], in_=raw[:].rearrange("p g j d -> p g d j"))
+            nc.vector.tensor_copy(out=grouped[:], in_=vraw[b][:].rearrange("p g j d -> p g d j"))
             vc = v_keep.tile([P, N_PASS * DH], U32, align_bytes=64)
             vs = v_keep.tile([P, N_PASS * DH], U8, align_bytes=64)
             nc.vector.quantize_mx(
@@ -159,22 +170,21 @@ def tile_multiheadattention_pa_kernel(tc, query, k, value, out):
             rp = ps_misc.tile([P, PACK * P], F32, tag="misc")
             for j in range(PACK):
                 nc.tensor.transpose(out=rp[:, j * P : (j + 1) * P], in_=r_t[i][:, j * P : (j + 1) * P], identity=ident_f[:])
-            rs = r_pool.tile([P, P, PACK], F32)
-            nc.scalar.copy(out=rs[:], in_=rp[:].rearrange("p (j q) -> p q j", j=PACK))
+            rs = r_pool.tile([P, PACK, P], F32)
+            nc.scalar.copy(out=rs[:].rearrange("p j q -> p (j q)"), in_=rp[:])
             r_sb[i] = rs
 
-        def weights(i):
-            wt = w_pool.tile([P, H, P, PACK], BF16, align_bytes=64)
-            w[i] = wt
-            ev = e[i][:].rearrange("p j h q -> p h q j")
-            for eng, h0, h1 in ((nc.gpsimd, 0, HEADS_ON_GPSIMD), (nc.vector, HEADS_ON_GPSIMD, H)):
-                if h1 > h0:
-                    eng.tensor_tensor(
-                        out=wt[:, h0:h1],
-                        in0=ev[:, h0:h1],
-                        in1=r_sb[i][:].unsqueeze(1).to_broadcast([P, h1 - h0, P, PACK]),
-                        op=ALU.mult,
-                    )
+        def weights(i, eng, h0, h1):
+            if h0 == 0:
+                wt = w_pool.tile([P, H, P, PACK], BF16, align_bytes=64)
+                w[i] = wt
+            for h in range(h0, h1):
+                eng.tensor_tensor(
+                    out=w[i][:, h].rearrange("p (c n) j -> p c j n", n=RUN),
+                    in0=e[i][:, :, h, :].rearrange("p j (c n) -> p c j n", n=RUN),
+                    in1=r_sb[i][:].rearrange("p j (c n) -> p c j n", n=RUN),
+                    op=ALU.mult,
+                )
 
         def quantise(i):
             cd = code_pool.tile([P, H * P], U32, align_bytes=64)
@@ -218,42 +228,45 @@ def tile_multiheadattention_pa_kernel(tc, query, k, value, out):
                 if s_need >= 2:
                     at(s_need - 2, prep_k, 0, g, j)
                 at(per_b - 16 + g * PACK + j, prep_k, 1, g, j)
-            at(per_b - 20 + g * PACK, load_k, 1, g)
+            at(per_b - 20 + g * PACK, load_k, 1, g, 1)
         for b in range(B):
             for t in range(QT):
                 if (b, t) != (0, 0):
                     at(b * per_b + t * 16 - 3, prep_q, b, t)
-        at(per_b - 18, load_q, 1)
+        at(per_b - 18, load_q, 1, 0, QT)
+        at(per_b - 18, load_v, 1)
         at(per_b - 14, prep_v, 1)
 
-        load_k(0, 0)
-        load_q(0)
-        load_k(0, 1)
+        load_q(0, 0, 1)
+        load_k(0, 0, PACK)
+        load_q(0, 1, QT)
+        load_k(0, 1, 1)
+        load_v(0)
         prep_q(0, 0)
         prep_k(0, 0, 0)
         prep_k(0, 0, 1)
-        prep_v(0)
-        at(2, load_k, 0, 2)
-        at(6, load_k, 0, 3)
+        at(2, load_k, 0, 2, 1)
+        at(6, load_k, 0, 3, 1)
+        at(9, prep_v, 0)
 
-        for s in range(N_BLOCK * PACK + 16):
-            i, j = s // PACK, s % PACK
-            if i < N_BLOCK:
-                scores(i, j)
-            s1 = s - 11
-            if s1 >= 0 and s1 % PACK == 0 and s1 // PACK < N_BLOCK:
-                recip_back(s1 // PACK)
-                weights(s1 // PACK)
-            s2 = s - SUM_LAG
-            if 0 <= s2 < N_BLOCK * PACK:
-                head_sum(s2 // PACK, s2 % PACK)
-                if s2 % (2 * PACK) == 2 * PACK - 1:
-                    log_recip(s2 // PACK)
-            s3 = s - 15
-            if s3 >= 0 and s3 % PACK == 0 and s3 // PACK < N_BLOCK:
-                quantise(s3 // PACK)
-                b, t, g = where(s3 // PACK)
+        for m in range(N_BLOCK // 2):
+            s0 = 2 * PACK * m
+            for n in range(2 * PACK):
+                at(s0 + n + SUM_LAG, head_sum, 2 * m + n // PACK, n % PACK)
+            at(s0 + 2 * PACK - 1 + SUM_LAG, log_recip, 2 * m + 1)
+            for n in range(2):
+                i = 2 * m + n
+                at(s0 + BACK_AT[n], recip_back, i)
+                hg = HEADS_ON_GPSIMD if i < N_BLOCK - TAIL_BLOCKS else TAIL_HEADS_ON_GPSIMD
+                at(s0 + BACK_AT[n], weights, i, nc.gpsimd, 0, hg)
+                at(s0 + VMUL_AT[n], weights, i, nc.vector, hg, H)
+                at(s0 + QUANT_AT[n], quantise, i)
+                b, t, g = where(i)
                 if g == N_PASS - 1:
-                    context(b, t)
+                    at(s0 + QUANT_AT[n] + CONTEXT_LAG, context, b, t)
+
+        for s in range(max(extra) + 1):
+            if s < N_BLOCK * PACK:
+                scores(s // PACK, s % PACK)
             for fn, args in extra.get(s, []):
                 fn(*args)

@@ -23,13 +23,14 @@ QH = 64
 N_BLOCK = B * QT * N_PASS
 RUN = 4
 SUM_LAG = 3
+SKEW = 1
 BACK_AT = (14, 16)
 QUANT_AT = (20, 24)
 CONTEXT_LAG = 4
 TAIL_BLOCKS = 4
 TAIL_HEADS_ON_GPSIMD = 3
 VMUL_AT = (18, 22)
-HEADS_ON_GPSIMD = 6
+HEADS_ON_GPSIMD = 5
 MANUAL = True
 
 
@@ -60,7 +61,7 @@ def tile_multiheadattention_pa_kernel(tc, query, k, value, out):
         ident_f = const.tile([P, P], F32)
         make_identity(nc, ident_f[:])
 
-        kraw, qraw, vraw, k_t, q_t = {}, {}, {}, {}, {}
+        kraw, qraw, vraw, k_t, q_t, bank = {}, {}, {}, {}, {}, {}
         v_codes, v_scales = {}, {}
         e, sum_t, r_t, r_sb, w, codes, scales = {}, {}, {}, {}, {}, {}, {}
 
@@ -114,34 +115,39 @@ def tile_multiheadattention_pa_kernel(tc, query, k, value, out):
             v_codes[b] = vc
             v_scales[b] = vs
 
-        def scores(i, j):
+        def scores(n):
+            i, j, qh = n // (2 * PACK), (n // 2) % PACK, n % 2
             b, t, g = where(i)
-            if j == 0:
+            if j == 0 and qh == 0:
                 et = e_pool.tile([P, PACK, H, P], F32)
                 e[i] = et
-            for qh in range(P // QH):
-                cols = slice(qh * QH, (qh + 1) * QH)
-                sc = ps_sc.tile([P, H * QH], F32)
-                for h in range(H):
-                    nc.tensor.matmul(
-                        out=sc[:, h * QH : (h + 1) * QH],
-                        lhsT=k_t[(b, g)][:, j, h, :],
-                        rhs=q_t[(b, t)][:, h, cols],
-                        start=True,
-                        stop=True,
-                    )
-                top = c_pool.tile([P, QH], F32)
-                nc.vector.tensor_reduce(
-                    out=top[:], in_=sc[:].rearrange("p (h q) -> p q h", h=H), axis=mybir.AxisListType.X, op=ALU.max
+            sc = ps_sc.tile([P, H * QH], F32)
+            for h in range(H):
+                nc.tensor.matmul(
+                    out=sc[:, h * QH : (h + 1) * QH],
+                    lhsT=k_t[(b, g)][:, j, h, :],
+                    rhs=q_t[(b, t)][:, h, qh * QH : (qh + 1) * QH],
+                    start=True,
+                    stop=True,
                 )
-                nc.vector.tensor_tensor(
-                    out=e[i][:, j, :, cols],
-                    in0=sc[:].rearrange("p (h q) -> p h q", h=H),
-                    in1=top[:].unsqueeze(1).to_broadcast([P, H, QH]),
-                    op=ALU.subtract,
-                )
-            flat = e[i][:, j].rearrange("p h q -> p (h q)")
-            nc.scalar.activation(out=flat, in_=flat, func=ACT.Exp, scale=DH**-0.5)
+            top = c_pool.tile([P, QH], F32)
+            nc.vector.tensor_reduce(
+                out=top[:], in_=sc[:].rearrange("p (h q) -> p q h", h=H), axis=mybir.AxisListType.X, op=ALU.max
+            )
+            bank[n] = (sc, top)
+
+        def shift(n):
+            i, j, qh = n // (2 * PACK), (n // 2) % PACK, n % 2
+            sc, top = bank[n]
+            nc.vector.tensor_tensor(
+                out=e[i][:, j, :, qh * QH : (qh + 1) * QH],
+                in0=sc[:].rearrange("p (h q) -> p h q", h=H),
+                in1=top[:].unsqueeze(1).to_broadcast([P, H, QH]),
+                op=ALU.subtract,
+            )
+            if qh == 1:
+                flat = e[i][:, j].rearrange("p h q -> p (h q)")
+                nc.scalar.activation(out=flat, in_=flat, func=ACT.Exp, scale=DH**-0.5)
 
         def head_sum(i, j):
             if j == 0:
@@ -265,8 +271,12 @@ def tile_multiheadattention_pa_kernel(tc, query, k, value, out):
                 if g == N_PASS - 1:
                     at(s0 + QUANT_AT[n] + CONTEXT_LAG, context, b, t)
 
+        n_bank = 2 * N_BLOCK * PACK
         for s in range(max(extra) + 1):
-            if s < N_BLOCK * PACK:
-                scores(s // PACK, s % PACK)
+            for n in (2 * s, 2 * s + 1):
+                if n < n_bank:
+                    scores(n)
+                if 0 <= n - SKEW < n_bank:
+                    shift(n - SKEW)
             for fn, args in extra.get(s, []):
                 fn(*args)

@@ -30,7 +30,7 @@ CONTEXT_LAG = 4
 TAIL_BLOCKS = 4
 TAIL_HEADS_ON_GPSIMD = 3
 VMUL_AT = (18, 22)
-HEADS_ON_GPSIMD = 5
+HEADS_ON_GPSIMD = 7
 MANUAL = True
 
 

@@ -18,41 +18,50 @@ P = 128
 PACK = 4
 K_PASS = P * PACK
 N_PASS = TV // K_PASS
-QT = TQ // P
-QH = 64
-N_BLOCK = B * QT * N_PASS
+N_QT = TQ // P
+QB = 64
+BANKS = P // QB
+STEPS_QT = N_PASS * PACK
+STEPS_B = N_QT * STEPS_QT
+N_STEP = B * STEPS_B
+N_BLOCK = N_STEP // PACK
 RUN = 4
+
+LOAD_Q_AHEAD = 9
+LOAD_K_AHEAD = 7
+PREP_Q_AHEAD = 3
+PREP_K_AHEAD = 3
+PREP_V_LAG = 9
 SUM_LAG = 3
-SKEW = 1
-BACK_AT = (14, 16)
-QUANT_AT = (20, 24)
-CONTEXT_LAG = 4
+RECIP_LAG = SUM_LAG + 2 * PACK - 1
+BACK_LAG = RECIP_LAG + 4
+VECTOR_SHARE_LAG = 18
+QUANT_LAG = 20
+CONTEXT_LAG = QUANT_LAG + 4
+GPSIMD_HEADS = 7
 TAIL_BLOCKS = 4
-TAIL_HEADS_ON_GPSIMD = 3
-VMUL_AT = (18, 22)
-HEADS_ON_GPSIMD = 7
-MANUAL = True
+TAIL_GPSIMD_HEADS = 3
 
 
 def tile_multiheadattention_pa_kernel(tc, query, k, value, out):
     nc = tc.nc
     with ExitStack() as ctx:
-        if MANUAL:
-            ctx.enter_context(tc.manual_schedule())
+        ctx.enter_context(tc.manual_schedule())
         const = ctx.enter_context(tc.tile_pool(name="const", bufs=1))
-        kraw_pool = ctx.enter_context(tc.tile_pool(name="kraw", bufs=2))
-        qraw_pool = ctx.enter_context(tc.tile_pool(name="qraw", bufs=1))
-        kt_pool = ctx.enter_context(tc.tile_pool(name="kt", bufs=5))
+        kraw_pool = ctx.enter_context(tc.tile_pool(name="kraw", bufs=LOAD_K_AHEAD))
+        qraw_pool = ctx.enter_context(tc.tile_pool(name="qraw", bufs=2))
+        kt_pool = ctx.enter_context(tc.tile_pool(name="kt", bufs=N_PASS))
         qt_pool = ctx.enter_context(tc.tile_pool(name="qt", bufs=2))
         v_stage = ctx.enter_context(tc.tile_pool(name="vstage", bufs=1))
         v_keep = ctx.enter_context(tc.tile_pool(name="vkeep", bufs=2))
         e_pool = ctx.enter_context(tc.tile_pool(name="e", bufs=5))
-        c_pool = ctx.enter_context(tc.tile_pool(name="c", bufs=4))
+        top_pool = ctx.enter_context(tc.tile_pool(name="top", bufs=4))
         r_pool = ctx.enter_context(tc.tile_pool(name="r", bufs=2))
+        rs_pool = ctx.enter_context(tc.tile_pool(name="rs", bufs=3))
         w_pool = ctx.enter_context(tc.tile_pool(name="w", bufs=2))
-        code_pool = ctx.enter_context(tc.tile_pool(name="code", bufs=5))
+        code_pool = ctx.enter_context(tc.tile_pool(name="code", bufs=N_PASS + 1))
         o_pool = ctx.enter_context(tc.tile_pool(name="o", bufs=1))
-        ps_sc = ctx.enter_context(tc.psum_pool(name="ps_sc", bufs=3))
+        ps_score = ctx.enter_context(tc.psum_pool(name="ps_score", bufs=3))
         ps_sum = ctx.enter_context(tc.psum_pool(name="ps_sum", bufs=3))
         ps_misc = ctx.enter_context(tc.psum_pool(name="ps_misc", bufs=2))
 
@@ -61,48 +70,44 @@ def tile_multiheadattention_pa_kernel(tc, query, k, value, out):
         ident_f = const.tile([P, P], F32)
         make_identity(nc, ident_f[:])
 
-        kraw, qraw, vraw, k_t, q_t, bank = {}, {}, {}, {}, {}, {}
-        v_codes, v_scales = {}, {}
-        e, sum_t, r_t, r_sb, w, codes, scales = {}, {}, {}, {}, {}, {}, {}
+        kraw, qraw, vraw, k_t, q_t, v_codes, v_scales = {}, {}, {}, {}, {}, {}, {}
+        bank, e, sum_t, r_t, r_sb, w, codes, scales = {}, {}, {}, {}, {}, {}, {}, {}
 
-        def where(i):
-            return i // (QT * N_PASS), (i // N_PASS) % QT, i % N_PASS
+        def place(s):
+            return s // STEPS_B, (s % STEPS_B) // STEPS_QT, (s % STEPS_QT) // PACK, s % PACK
 
-        def load_k(b, g, pieces):
-            raw = kraw_pool.tile([P, PACK, H * DH], BF16)
+        def load_q(b, t):
+            raw = qraw_pool.tile([P, H * DH], BF16)
+            nc.sync.dma_start(out=raw[:], in_=query[b, t * P : (t + 1) * P, :])
+            qraw[(b, t)] = raw
+
+        def load_k(b, g, j):
+            raw = kraw_pool.tile([P, H * DH], BF16)
             rows = k[b, g * K_PASS : (g + 1) * K_PASS, :].rearrange("(p j) c -> p j c", j=PACK)
-            step = PACK // pieces
-            for n in range(pieces):
-                nc.sync.dma_start(out=raw[:, n * step : (n + 1) * step, :], in_=rows[:, n * step : (n + 1) * step, :])
-            kraw[(b, g)] = raw
-
-        def load_q(b, t0, t1):
-            if t0 == 0:
-                raw = qraw_pool.tile([P, QT, H * DH], BF16)
-                qraw[b] = raw
-            nc.sync.dma_start(out=qraw[b][:, t0:t1, :], in_=query[b].rearrange("(t p) c -> p t c", p=P)[:, t0:t1, :])
+            nc.sync.dma_start(out=raw[:], in_=rows[:, j, :])
+            kraw[(b, g, j)] = raw
 
         def load_v(b):
             raw = v_stage.tile([P, N_PASS, PACK, DH], BF16)
             nc.sync.dma_start(out=raw[:], in_=value[b].rearrange("(g p j) d -> p g j d", p=P, j=PACK))
             vraw[b] = raw
 
+        def transpose_heads(raw, dst):
+            tp = ps_misc.tile([P, H, P], BF16, tag="misc")
+            for h in range(H):
+                nc.tensor.transpose(out=tp[:, h, :], in_=raw[:, h * DH : (h + 1) * DH], identity=ident_bf[:])
+            nc.scalar.copy(out=dst, in_=tp[:])
+
+        def prep_q(b, t):
+            qt = qt_pool.tile([P, H, P], BF16)
+            transpose_heads(qraw[(b, t)], qt[:])
+            q_t[(b, t)] = qt
+
         def prep_k(b, g, j):
             if j == 0:
                 kt = kt_pool.tile([P, PACK, H, P], BF16)
                 k_t[(b, g)] = kt
-            tp = ps_misc.tile([P, H, P], BF16, tag="misc")
-            for h in range(H):
-                nc.tensor.transpose(out=tp[:, h, :], in_=kraw[(b, g)][:, j, h * DH : (h + 1) * DH], identity=ident_bf[:])
-            nc.scalar.copy(out=k_t[(b, g)][:, j], in_=tp[:])
-
-        def prep_q(b, t):
-            qt = qt_pool.tile([P, H, P], BF16)
-            tp = ps_misc.tile([P, H, P], BF16, tag="misc")
-            for h in range(H):
-                nc.tensor.transpose(out=tp[:, h, :], in_=qraw[b][:, t, h * DH : (h + 1) * DH], identity=ident_bf[:])
-            nc.scalar.copy(out=qt[:], in_=tp[:])
-            q_t[(b, t)] = qt
+            transpose_heads(kraw[(b, g, j)], k_t[(b, g)][:, j])
 
         def prep_v(b):
             grouped = v_stage.tile([P, N_PASS, DH, PACK], BF16, align_bytes=64)
@@ -116,40 +121,42 @@ def tile_multiheadattention_pa_kernel(tc, query, k, value, out):
             v_scales[b] = vs
 
         def scores(n):
-            i, j, qh = n // (2 * PACK), (n // 2) % PACK, n % 2
-            b, t, g = where(i)
-            if j == 0 and qh == 0:
+            s, half = n // BANKS, n % BANKS
+            b, t, g, j = place(s)
+            if j == 0 and half == 0:
                 et = e_pool.tile([P, PACK, H, P], F32)
-                e[i] = et
-            sc = ps_sc.tile([P, H * QH], F32)
+                e[s // PACK] = et
+            sc = ps_score.tile([P, H * QB], F32)
             for h in range(H):
                 nc.tensor.matmul(
-                    out=sc[:, h * QH : (h + 1) * QH],
+                    out=sc[:, h * QB : (h + 1) * QB],
                     lhsT=k_t[(b, g)][:, j, h, :],
-                    rhs=q_t[(b, t)][:, h, qh * QH : (qh + 1) * QH],
+                    rhs=q_t[(b, t)][:, h, half * QB : (half + 1) * QB],
                     start=True,
                     stop=True,
                 )
-            top = c_pool.tile([P, QH], F32)
+            top = top_pool.tile([P, QB], F32)
             nc.vector.tensor_reduce(
                 out=top[:], in_=sc[:].rearrange("p (h q) -> p q h", h=H), axis=mybir.AxisListType.X, op=ALU.max
             )
             bank[n] = (sc, top)
 
-        def shift(n):
-            i, j, qh = n // (2 * PACK), (n // 2) % PACK, n % 2
+        def shift_exp(n):
+            s, half = n // BANKS, n % BANKS
             sc, top = bank[n]
+            et = e[s // PACK]
             nc.vector.tensor_tensor(
-                out=e[i][:, j, :, qh * QH : (qh + 1) * QH],
+                out=et[:, s % PACK, :, half * QB : (half + 1) * QB],
                 in0=sc[:].rearrange("p (h q) -> p h q", h=H),
-                in1=top[:].unsqueeze(1).to_broadcast([P, H, QH]),
+                in1=top[:].unsqueeze(1).to_broadcast([P, H, QB]),
                 op=ALU.subtract,
             )
-            if qh == 1:
-                flat = e[i][:, j].rearrange("p h q -> p (h q)")
+            if half == BANKS - 1:
+                flat = et[:, s % PACK].rearrange("p h q -> p (h q)")
                 nc.scalar.activation(out=flat, in_=flat, func=ACT.Exp, scale=DH**-0.5)
 
-        def head_sum(i, j):
+        def head_sum(s):
+            i, j = s // PACK, s % PACK
             if j == 0:
                 st = ps_sum.tile([P, PACK * P], F32)
                 sum_t[i] = st
@@ -163,28 +170,29 @@ def tile_multiheadattention_pa_kernel(tc, query, k, value, out):
                     stop=(h == H - 1),
                 )
 
-        def log_recip(i):
+        def reciprocal(m):
             rt = r_pool.tile([P, 2, PACK * P], F32)
             for n in range(2):
-                nc.scalar.activation(out=rt[:, n], in_=sum_t[i - 1 + n][:], func=ACT.Ln)
+                nc.scalar.activation(out=rt[:, n], in_=sum_t[2 * m + n][:], func=ACT.Ln)
             flat = rt[:].rearrange("p n c -> p (n c)")
             nc.scalar.activation(out=flat, in_=flat, func=ACT.Exp, scale=-1.0)
-            r_t[i - 1] = rt[:, 0]
-            r_t[i] = rt[:, 1]
+            r_t[m] = rt
 
-        def recip_back(i):
+        def reciprocal_back(i):
             rp = ps_misc.tile([P, PACK * P], F32, tag="misc")
             for j in range(PACK):
-                nc.tensor.transpose(out=rp[:, j * P : (j + 1) * P], in_=r_t[i][:, j * P : (j + 1) * P], identity=ident_f[:])
-            rs = r_pool.tile([P, PACK, P], F32)
+                nc.tensor.transpose(
+                    out=rp[:, j * P : (j + 1) * P], in_=r_t[i // 2][:, i % 2, j * P : (j + 1) * P], identity=ident_f[:]
+                )
+            rs = rs_pool.tile([P, PACK, P], F32)
             nc.scalar.copy(out=rs[:].rearrange("p j q -> p (j q)"), in_=rp[:])
             r_sb[i] = rs
 
-        def weights(i, eng, h0, h1):
-            if h0 == 0:
-                wt = w_pool.tile([P, H, P, PACK], BF16, align_bytes=64)
-                w[i] = wt
-            for h in range(h0, h1):
+        def gpsimd_heads(i):
+            return GPSIMD_HEADS if i < N_BLOCK - TAIL_BLOCKS else TAIL_GPSIMD_HEADS
+
+        def weights(i, eng, heads):
+            for h in heads:
                 eng.tensor_tensor(
                     out=w[i][:, h].rearrange("p (c n) j -> p c j n", n=RUN),
                     in0=e[i][:, :, h, :].rearrange("p j (c n) -> p c j n", n=RUN),
@@ -204,14 +212,13 @@ def tile_multiheadattention_pa_kernel(tc, query, k, value, out):
         def context(b, t):
             res = o_pool.tile([P, H * DH], F32)
             per_bank = 4
-            for half in range(H // per_bank):
+            for first in range(0, H, per_bank):
                 acc = ps_misc.tile([P, per_bank * DH], F32, tag="misc")
-                for hh in range(per_bank):
-                    h = half * per_bank + hh
+                for h in range(first, first + per_bank):
                     for g in range(N_PASS):
-                        i = (b * QT + t) * N_PASS + g
+                        i = (b * N_QT + t) * N_PASS + g
                         nc.tensor.matmul_mx(
-                            out=acc[:, hh * DH : (hh + 1) * DH],
+                            out=acc[:, (h - first) * DH : (h - first + 1) * DH],
                             lhsT=codes[i][:, h * P : (h + 1) * P].bitcast(FP8X4),
                             lhsT_scale=scales[i][:, h * P : (h + 1) * P],
                             rhs=v_codes[b][:, g * DH : (g + 1) * DH].bitcast(FP8X4),
@@ -219,64 +226,49 @@ def tile_multiheadattention_pa_kernel(tc, query, k, value, out):
                             start=(g == 0),
                             stop=(g == N_PASS - 1),
                         )
-                nc.scalar.copy(out=res[:, half * per_bank * DH : (half + 1) * per_bank * DH], in_=acc[:])
+                nc.scalar.copy(out=res[:, first * DH : (first + per_bank) * DH], in_=acc[:])
             nc.sync.dma_start(out=out[b, t * P : (t + 1) * P, :], in_=res[:])
 
-        extra = {}
+        def starts(s, period):
+            return 0 <= s < N_STEP and s % period == 0
 
-        def at(s, fn, *args):
-            extra[s] = extra.get(s, []) + [(fn, args)]
-
-        per_b = QT * N_PASS * PACK
-        for g in range(N_PASS):
-            for j in range(PACK):
-                s_need = g * PACK + j
-                if s_need >= 2:
-                    at(s_need - 2, prep_k, 0, g, j)
-                at(per_b - 16 + g * PACK + j, prep_k, 1, g, j)
-            at(per_b - 20 + g * PACK, load_k, 1, g, 1)
-        for b in range(B):
-            for t in range(QT):
-                if (b, t) != (0, 0):
-                    at(b * per_b + t * 16 - 3, prep_q, b, t)
-        at(per_b - 18, load_q, 1, 0, QT)
-        at(per_b - 18, load_v, 1)
-        at(per_b - 14, prep_v, 1)
-
-        load_q(0, 0, 1)
-        load_k(0, 0, PACK)
-        load_q(0, 1, QT)
-        load_k(0, 1, 1)
-        load_v(0)
-        prep_q(0, 0)
-        prep_k(0, 0, 0)
-        prep_k(0, 0, 1)
-        at(2, load_k, 0, 2, 1)
-        at(6, load_k, 0, 3, 1)
-        at(9, prep_v, 0)
-
-        for m in range(N_BLOCK // 2):
-            s0 = 2 * PACK * m
-            for n in range(2 * PACK):
-                at(s0 + n + SUM_LAG, head_sum, 2 * m + n // PACK, n % PACK)
-            at(s0 + 2 * PACK - 1 + SUM_LAG, log_recip, 2 * m + 1)
-            for n in range(2):
-                i = 2 * m + n
-                at(s0 + BACK_AT[n], recip_back, i)
-                hg = HEADS_ON_GPSIMD if i < N_BLOCK - TAIL_BLOCKS else TAIL_HEADS_ON_GPSIMD
-                at(s0 + BACK_AT[n], weights, i, nc.gpsimd, 0, hg)
-                at(s0 + VMUL_AT[n], weights, i, nc.vector, hg, H)
-                at(s0 + QUANT_AT[n], quantise, i)
-                b, t, g = where(i)
-                if g == N_PASS - 1:
-                    at(s0 + QUANT_AT[n] + CONTEXT_LAG, context, b, t)
-
-        n_bank = 2 * N_BLOCK * PACK
-        for s in range(max(extra) + 1):
-            for n in (2 * s, 2 * s + 1):
-                if n < n_bank:
+        for s in range(-LOAD_Q_AHEAD, N_STEP + CONTEXT_LAG):
+            for n in range(BANKS * s, BANKS * (s + 1)):
+                if 0 <= n < BANKS * N_STEP:
                     scores(n)
-                if 0 <= n - SKEW < n_bank:
-                    shift(n - SKEW)
-            for fn, args in extra.get(s, []):
-                fn(*args)
+                if 0 <= n - 1 < BANKS * N_STEP:
+                    shift_exp(n - 1)
+            if starts(s + LOAD_Q_AHEAD, STEPS_QT):
+                b, t, g, j = place(s + LOAD_Q_AHEAD)
+                load_q(b, t)
+                if t == 0:
+                    load_v(b)
+            if starts(s + LOAD_K_AHEAD, 1) and place(s + LOAD_K_AHEAD)[1] == 0:
+                b, t, g, j = place(s + LOAD_K_AHEAD)
+                load_k(b, g, j)
+            if starts(s + PREP_Q_AHEAD, STEPS_QT):
+                b, t, g, j = place(s + PREP_Q_AHEAD)
+                prep_q(b, t)
+            if starts(s + PREP_K_AHEAD, 1) and place(s + PREP_K_AHEAD)[1] == 0:
+                b, t, g, j = place(s + PREP_K_AHEAD)
+                prep_k(b, g, j)
+            if starts(s - PREP_V_LAG, STEPS_B):
+                prep_v((s - PREP_V_LAG) // STEPS_B)
+            if starts(s - BACK_LAG, PACK):
+                i = (s - BACK_LAG) // PACK
+                reciprocal_back(i)
+                wt = w_pool.tile([P, H, P, PACK], BF16, align_bytes=64)
+                w[i] = wt
+                weights(i, nc.gpsimd, range(gpsimd_heads(i)))
+            if starts(s - SUM_LAG, 1):
+                head_sum(s - SUM_LAG)
+            if starts(s - RECIP_LAG, 2 * PACK):
+                reciprocal((s - RECIP_LAG) // (2 * PACK))
+            if starts(s - VECTOR_SHARE_LAG, PACK):
+                i = (s - VECTOR_SHARE_LAG) // PACK
+                weights(i, nc.vector, range(gpsimd_heads(i), H))
+            if starts(s - QUANT_LAG, PACK):
+                quantise((s - QUANT_LAG) // PACK)
+            if starts(s - CONTEXT_LAG - (STEPS_QT - PACK), STEPS_QT):
+                b, t, g, j = place(s - CONTEXT_LAG)
+                context(b, t)

@@ -25,7 +25,6 @@ STEPS_QT = N_PASS * PACK
 STEPS_B = N_QT * STEPS_QT
 N_STEP = B * STEPS_B
 N_BLOCK = N_STEP // PACK
-RUN = 4
 
 LOAD_Q_AHEAD = 9
 LOAD_K_AHEAD = 7
@@ -174,8 +173,6 @@ def tile_multiheadattention_pa_kernel(tc, query, k, value, out):
             rt = r_pool.tile([P, 2, PACK * P], F32)
             for n in range(2):
                 nc.scalar.activation(out=rt[:, n], in_=sum_t[2 * m + n][:], func=ACT.Ln)
-            flat = rt[:].rearrange("p n c -> p (n c)")
-            nc.scalar.activation(out=flat, in_=flat, func=ACT.Exp, scale=-1.0)
             r_t[m] = rt
 
         def reciprocal_back(i):
@@ -184,8 +181,10 @@ def tile_multiheadattention_pa_kernel(tc, query, k, value, out):
                 nc.tensor.transpose(
                     out=rp[:, j * P : (j + 1) * P], in_=r_t[i // 2][:, i % 2, j * P : (j + 1) * P], identity=ident_f[:]
                 )
-            rs = rs_pool.tile([P, PACK, P], F32)
-            nc.scalar.copy(out=rs[:].rearrange("p j q -> p (j q)"), in_=rp[:])
+            rs = rs_pool.tile([P, P, PACK], F32)
+            nc.scalar.activation(
+                out=rs[:], in_=rp[:].rearrange("p (j q) -> p q j", j=PACK), func=ACT.Exp, scale=-1.0
+            )
             r_sb[i] = rs
 
         def gpsimd_heads(i):
@@ -194,9 +193,9 @@ def tile_multiheadattention_pa_kernel(tc, query, k, value, out):
         def weights(i, eng, heads):
             for h in heads:
                 eng.tensor_tensor(
-                    out=w[i][:, h].rearrange("p (c n) j -> p c j n", n=RUN),
-                    in0=e[i][:, :, h, :].rearrange("p j (c n) -> p c j n", n=RUN),
-                    in1=r_sb[i][:].rearrange("p j (c n) -> p c j n", n=RUN),
+                    out=w[i][:, h],
+                    in0=e[i][:, :, h, :].rearrange("p j q -> p q j"),
+                    in1=r_sb[i][:],
                     op=ALU.mult,
                 )
 

@@ -20,27 +20,33 @@ K_PASS = P * PACK
 N_PASS = TV // K_PASS
 N_QT = TQ // P
 QB = 64
-BANKS = P // QB
-STEPS_QT = N_PASS * PACK
+QC = P // PACK
+HALVES = P // QB
+CHUNKS = QB // QC
+BANKS = 2
+STEPS_U = PACK // BANKS
+STEPS_K = HALVES * STEPS_U
+STEPS_QT = N_PASS * STEPS_K
 STEPS_B = N_QT * STEPS_QT
 N_STEP = B * STEPS_B
-N_BLOCK = N_STEP // PACK
+N_BLOCK = N_STEP // STEPS_K
 
-LOAD_Q_AHEAD = 9
-LOAD_K_AHEAD = 7
-PREP_Q_AHEAD = 3
-PREP_K_AHEAD = 3
+LOAD_Q_AHEAD = 11
+LOAD_K_AHEAD = 9
+PREP_Q_AHEAD = 5
+PREP_K_AHEAD = 5
 PREP_V_LAG = 9
-SUM_LAG = 3
-RECIP_LAG = SUM_LAG + 2 * PACK - 1
+EXP_LAG = STEPS_U
+SUM_LAG = EXP_LAG + 2
+RECIP_LAG = SUM_LAG + 2 * STEPS_K - 1
 BACK_LAG = RECIP_LAG + 4
-VECTOR_SHARE_LAG = 18
-QUANT_LAG = 20
+VECTOR_SHARE_LAG = BACK_LAG + 4
+QUANT_LAG = BACK_LAG + 6
 CONTEXT_LAG = QUANT_LAG + 4
-GPSIMD_HEADS = 7
+HEAD_GROUP = 4
+GPSIMD_HEADS = 8
 TAIL_BLOCKS = 4
-TAIL_GPSIMD_HEADS = 3
-
+TAIL_GPSIMD_HEADS = 4
 
 def tile_multiheadattention_pa_kernel(tc, query, k, value, out):
     nc = tc.nc
@@ -53,7 +59,8 @@ def tile_multiheadattention_pa_kernel(tc, query, k, value, out):
         qt_pool = ctx.enter_context(tc.tile_pool(name="qt", bufs=2))
         v_stage = ctx.enter_context(tc.tile_pool(name="vstage", bufs=1))
         v_keep = ctx.enter_context(tc.tile_pool(name="vkeep", bufs=2))
-        e_pool = ctx.enter_context(tc.tile_pool(name="e", bufs=5))
+        shift_pool = ctx.enter_context(tc.tile_pool(name="shift", bufs=3))
+        e_pool = ctx.enter_context(tc.tile_pool(name="e", bufs=10))
         top_pool = ctx.enter_context(tc.tile_pool(name="top", bufs=4))
         r_pool = ctx.enter_context(tc.tile_pool(name="r", bufs=2))
         rs_pool = ctx.enter_context(tc.tile_pool(name="rs", bufs=3))
@@ -70,10 +77,10 @@ def tile_multiheadattention_pa_kernel(tc, query, k, value, out):
         make_identity(nc, ident_f[:])
 
         kraw, qraw, vraw, k_t, q_t, v_codes, v_scales = {}, {}, {}, {}, {}, {}, {}
-        bank, e, sum_t, r_t, r_sb, w, codes, scales = {}, {}, {}, {}, {}, {}, {}, {}
+        bank, shift, e, sum_t, r_t, r_sb, w, codes, scales = {}, {}, {}, {}, {}, {}, {}, {}, {}
 
         def place(s):
-            return s // STEPS_B, (s % STEPS_B) // STEPS_QT, (s % STEPS_QT) // PACK, s % PACK
+            return s // STEPS_B, (s % STEPS_B) // STEPS_QT, (s % STEPS_QT) // STEPS_K, s % STEPS_K
 
         def load_q(b, t):
             raw = qraw_pool.tile([P, H * DH], BF16)
@@ -120,11 +127,12 @@ def tile_multiheadattention_pa_kernel(tc, query, k, value, out):
             v_scales[b] = vs
 
         def scores(n):
-            s, half = n // BANKS, n % BANKS
-            b, t, g, j = place(s)
-            if j == 0 and half == 0:
-                et = e_pool.tile([P, PACK, H, P], F32)
-                e[s // PACK] = et
+            u, j = n // PACK, n % PACK
+            half = u % HALVES
+            b, t, g, first = place(u * STEPS_U)
+            if j == 0:
+                st = shift_pool.tile([P, PACK, H, QB], F32)
+                shift[u] = st
             sc = ps_score.tile([P, H * QB], F32)
             for h in range(H):
                 nc.tensor.matmul(
@@ -140,29 +148,37 @@ def tile_multiheadattention_pa_kernel(tc, query, k, value, out):
             )
             bank[n] = (sc, top)
 
-        def shift_exp(n):
-            s, half = n // BANKS, n % BANKS
+        def subtract(n):
             sc, top = bank[n]
-            et = e[s // PACK]
             nc.vector.tensor_tensor(
-                out=et[:, s % PACK, :, half * QB : (half + 1) * QB],
+                out=shift[n // PACK][:, n % PACK],
                 in0=sc[:].rearrange("p (h q) -> p h q", h=H),
                 in1=top[:].unsqueeze(1).to_broadcast([P, H, QB]),
                 op=ALU.subtract,
             )
-            if half == BANKS - 1:
-                flat = et[:, s % PACK].rearrange("p h q -> p (h q)")
-                nc.scalar.activation(out=flat, in_=flat, func=ACT.Exp, scale=DH**-0.5)
 
-        def head_sum(s):
-            i, j = s // PACK, s % PACK
-            if j == 0:
+        def exp_chunk(u, c):
+            if c == 0:
+                et = e_pool.tile([P, H, QB, PACK], F32)
+                e[u] = et
+            cols = slice(c * QC, (c + 1) * QC)
+            nc.scalar.activation(
+                out=e[u][:, :, cols, :],
+                in_=shift[u][:, :, :, cols].rearrange("p j h q -> p h q j"),
+                func=ACT.Exp,
+                scale=DH**-0.5,
+            )
+
+        def head_sum(u, c):
+            i, half = u // HALVES, u % HALVES
+            if half == 0 and c == 0:
                 st = ps_sum.tile([P, PACK * P], F32)
                 sum_t[i] = st
+            col = (half * CHUNKS + c) * P
             for h in range(H):
                 nc.tensor.matmul(
-                    out=sum_t[i][:, j * P : (j + 1) * P],
-                    lhsT=e[i][:, j, h, :],
+                    out=sum_t[i][:, col : col + P],
+                    lhsT=e[u][:, h, c * QC : (c + 1) * QC, :].rearrange("p q j -> p (q j)"),
                     rhs=ident_f[:],
                     is_transpose=True,
                     start=(h == 0),
@@ -177,13 +193,13 @@ def tile_multiheadattention_pa_kernel(tc, query, k, value, out):
 
         def reciprocal_back(i):
             rp = ps_misc.tile([P, PACK * P], F32, tag="misc")
-            for j in range(PACK):
+            for col in range(0, PACK * P, P):
                 nc.tensor.transpose(
-                    out=rp[:, j * P : (j + 1) * P], in_=r_t[i // 2][:, i % 2, j * P : (j + 1) * P], identity=ident_f[:]
+                    out=rp[:, col : col + P], in_=r_t[i // 2][:, i % 2, col : col + P], identity=ident_f[:]
                 )
             rs = rs_pool.tile([P, P, PACK], F32)
             nc.scalar.activation(
-                out=rs[:], in_=rp[:].rearrange("p (j q) -> p q j", j=PACK), func=ACT.Exp, scale=-1.0
+                out=rs[:].rearrange("p q j -> p (q j)"), in_=rp[:], func=ACT.Exp, scale=-1.0
             )
             r_sb[i] = rs
 
@@ -191,13 +207,19 @@ def tile_multiheadattention_pa_kernel(tc, query, k, value, out):
             return GPSIMD_HEADS if i < N_BLOCK - TAIL_BLOCKS else TAIL_GPSIMD_HEADS
 
         def weights(i, eng, heads):
-            for h in heads:
-                eng.tensor_tensor(
-                    out=w[i][:, h],
-                    in0=e[i][:, :, h, :].rearrange("p j q -> p q j"),
-                    in1=r_sb[i][:],
-                    op=ALU.mult,
-                )
+            for half in range(HALVES):
+                qs = slice(half * QB, (half + 1) * QB)
+                for h in range(heads.start, heads.stop, HEAD_GROUP):
+                    hs = slice(h, h + HEAD_GROUP)
+                    eng.tensor_tensor(
+                        out=w[i][:, hs, qs, :].rearrange("p h q j -> p h (q j)"),
+                        in0=e[i * HALVES + half][:, hs].rearrange("p h q j -> p h (q j)"),
+                        in1=r_sb[i][:, qs, :]
+                        .rearrange("p q j -> p (q j)")
+                        .unsqueeze(1)
+                        .to_broadcast([P, HEAD_GROUP, QB * PACK]),
+                        op=ALU.mult,
+                    )
 
         def quantise(i):
             cd = code_pool.tile([P, H * P], U32, align_bytes=64)
@@ -236,7 +258,9 @@ def tile_multiheadattention_pa_kernel(tc, query, k, value, out):
                 if 0 <= n < BANKS * N_STEP:
                     scores(n)
                 if 0 <= n - 1 < BANKS * N_STEP:
-                    shift_exp(n - 1)
+                    subtract(n - 1)
+            if starts(s - EXP_LAG, 1):
+                exp_chunk((s - EXP_LAG) // STEPS_U, (s - EXP_LAG) % STEPS_U)
             if starts(s + LOAD_Q_AHEAD, STEPS_QT):
                 b, t, g, j = place(s + LOAD_Q_AHEAD)
                 load_q(b, t)
@@ -253,21 +277,21 @@ def tile_multiheadattention_pa_kernel(tc, query, k, value, out):
                 prep_k(b, g, j)
             if starts(s - PREP_V_LAG, STEPS_B):
                 prep_v((s - PREP_V_LAG) // STEPS_B)
-            if starts(s - BACK_LAG, PACK):
-                i = (s - BACK_LAG) // PACK
+            if starts(s - BACK_LAG, STEPS_K):
+                i = (s - BACK_LAG) // STEPS_K
                 reciprocal_back(i)
                 wt = w_pool.tile([P, H, P, PACK], BF16, align_bytes=64)
                 w[i] = wt
                 weights(i, nc.gpsimd, range(gpsimd_heads(i)))
             if starts(s - SUM_LAG, 1):
-                head_sum(s - SUM_LAG)
-            if starts(s - RECIP_LAG, 2 * PACK):
-                reciprocal((s - RECIP_LAG) // (2 * PACK))
-            if starts(s - VECTOR_SHARE_LAG, PACK):
-                i = (s - VECTOR_SHARE_LAG) // PACK
+                head_sum((s - SUM_LAG) // STEPS_U, (s - SUM_LAG) % STEPS_U)
+            if starts(s - RECIP_LAG, 2 * STEPS_K):
+                reciprocal((s - RECIP_LAG) // (2 * STEPS_K))
+            if starts(s - VECTOR_SHARE_LAG, STEPS_K):
+                i = (s - VECTOR_SHARE_LAG) // STEPS_K
                 weights(i, nc.vector, range(gpsimd_heads(i), H))
-            if starts(s - QUANT_LAG, PACK):
-                quantise((s - QUANT_LAG) // PACK)
-            if starts(s - CONTEXT_LAG - (STEPS_QT - PACK), STEPS_QT):
+            if starts(s - QUANT_LAG, STEPS_K):
+                quantise((s - QUANT_LAG) // STEPS_K)
+            if starts(s - CONTEXT_LAG - (STEPS_QT - STEPS_K), STEPS_QT):
                 b, t, g, j = place(s - CONTEXT_LAG)
                 context(b, t)

@@ -38,11 +38,15 @@ PREP_K_AHEAD = 5
 PREP_V_LAG = 9
 EXP_LAG = STEPS_U
 SUM_LAG = EXP_LAG + 2
+SUM_WAIT = 2
 RECIP_LAG = SUM_LAG + 2 * STEPS_K - 1
 BACK_LAG = RECIP_LAG + 4
 VECTOR_SHARE_LAG = BACK_LAG + 4
 QUANT_LAG = BACK_LAG + 6
 CONTEXT_LAG = QUANT_LAG + 4
+CONTEXT_HEADS = 2
+CHUNKS_PAIR = 2 * HALVES * CHUNKS
+CLOCK_COLS = 256
 HEAD_GROUP = 4
 GPSIMD_HEADS = 8
 TAIL_BLOCKS = 4
@@ -67,8 +71,8 @@ def tile_multiheadattention_pa_kernel(tc, query, k, value, out):
         w_pool = ctx.enter_context(tc.tile_pool(name="w", bufs=2))
         code_pool = ctx.enter_context(tc.tile_pool(name="code", bufs=N_PASS + 1))
         o_pool = ctx.enter_context(tc.tile_pool(name="o", bufs=1))
-        ps_score = ctx.enter_context(tc.psum_pool(name="ps_score", bufs=3))
-        ps_sum = ctx.enter_context(tc.psum_pool(name="ps_sum", bufs=3))
+        ps_score = ctx.enter_context(tc.psum_pool(name="ps_score", bufs=4))
+        ps_sum = ctx.enter_context(tc.psum_pool(name="ps_sum", bufs=2))
         ps_misc = ctx.enter_context(tc.psum_pool(name="ps_misc", bufs=2))
 
         ident_bf = const.tile([P, P], BF16)
@@ -77,7 +81,7 @@ def tile_multiheadattention_pa_kernel(tc, query, k, value, out):
         make_identity(nc, ident_f[:])
 
         kraw, qraw, vraw, k_t, q_t, v_codes, v_scales = {}, {}, {}, {}, {}, {}, {}
-        bank, shift, e, sum_t, r_t, r_sb, w, codes, scales = {}, {}, {}, {}, {}, {}, {}, {}, {}
+        bank, shift, e, sum_t, r_t, r_sb, w, codes, scales, acc, res = {}, {}, {}, {}, {}, {}, {}, {}, {}, {}, {}
 
         def place(s):
             return s // STEPS_B, (s % STEPS_B) // STEPS_QT, (s % STEPS_QT) // STEPS_K, s % STEPS_K
@@ -134,6 +138,16 @@ def tile_multiheadattention_pa_kernel(tc, query, k, value, out):
                 st = shift_pool.tile([P, PACK, H, QB], F32)
                 shift[u] = st
             sc = ps_score.tile([P, H * QB], F32)
+            if b in v_codes:
+                nc.tensor.matmul_mx(
+                    out=sc[:, :CLOCK_COLS],
+                    lhsT=v_codes[b][:, :P].bitcast(FP8X4),
+                    lhsT_scale=v_scales[b][:, :P],
+                    rhs=v_codes[b][:, :CLOCK_COLS].bitcast(FP8X4),
+                    rhs_scale=v_scales[b][:, :CLOCK_COLS],
+                    start=True,
+                    stop=True,
+                )
             for h in range(H):
                 nc.tensor.matmul(
                     out=sc[:, h * QB : (h + 1) * QB],
@@ -230,37 +244,53 @@ def tile_multiheadattention_pa_kernel(tc, query, k, value, out):
             codes[i] = cd
             scales[i] = sl
 
-        def context(b, t):
-            res = o_pool.tile([P, H * DH], F32)
+        def context(b, t, part):
             per_bank = 4
-            for first in range(0, H, per_bank):
-                acc = ps_misc.tile([P, per_bank * DH], F32, tag="misc")
-                for h in range(first, first + per_bank):
-                    for g in range(N_PASS):
-                        i = (b * N_QT + t) * N_PASS + g
-                        nc.tensor.matmul_mx(
-                            out=acc[:, (h - first) * DH : (h - first + 1) * DH],
-                            lhsT=codes[i][:, h * P : (h + 1) * P].bitcast(FP8X4),
-                            lhsT_scale=scales[i][:, h * P : (h + 1) * P],
-                            rhs=v_codes[b][:, g * DH : (g + 1) * DH].bitcast(FP8X4),
-                            rhs_scale=v_scales[b][:, g * DH : (g + 1) * DH],
-                            start=(g == 0),
-                            stop=(g == N_PASS - 1),
-                        )
-                nc.scalar.copy(out=res[:, first * DH : (first + per_bank) * DH], in_=acc[:])
-            nc.sync.dma_start(out=out[b, t * P : (t + 1) * P, :], in_=res[:])
+            if part == 0:
+                rt = o_pool.tile([P, H * DH], F32)
+                res[(b, t)] = rt
+            for h in range(CONTEXT_HEADS * part, CONTEXT_HEADS * (part + 1)):
+                if h % per_bank == 0:
+                    at = ps_misc.tile([P, per_bank * DH], F32, tag="misc")
+                    acc[(b, t)] = at
+                for g in range(N_PASS):
+                    i = (b * N_QT + t) * N_PASS + g
+                    nc.tensor.matmul_mx(
+                        out=acc[(b, t)][:, h % per_bank * DH : (h % per_bank + 1) * DH],
+                        lhsT=codes[i][:, h * P : (h + 1) * P].bitcast(FP8X4),
+                        lhsT_scale=scales[i][:, h * P : (h + 1) * P],
+                        rhs=v_codes[b][:, g * DH : (g + 1) * DH].bitcast(FP8X4),
+                        rhs_scale=v_scales[b][:, g * DH : (g + 1) * DH],
+                        start=(g == 0),
+                        stop=(g == N_PASS - 1),
+                    )
+                if h % per_bank == per_bank - 1:
+                    first = (h - per_bank + 1) * DH
+                    nc.scalar.copy(out=res[(b, t)][:, first : (h + 1) * DH], in_=acc[(b, t)][:])
+            if CONTEXT_HEADS * (part + 1) == H:
+                nc.sync.dma_start(out=out[b, t * P : (t + 1) * P, :], in_=res[(b, t)][:])
+
+        def sum_step(x):
+            k = x % CHUNKS_PAIR
+            return x - k + SUM_LAG + max(k, SUM_WAIT + k // 2)
 
         def starts(s, period):
             return 0 <= s < N_STEP and s % period == 0
 
-        for s in range(-LOAD_Q_AHEAD, N_STEP + CONTEXT_LAG):
+        for s in range(-LOAD_Q_AHEAD, N_STEP + CONTEXT_LAG + H // CONTEXT_HEADS):
             for n in range(BANKS * s, BANKS * (s + 1)):
                 if 0 <= n < BANKS * N_STEP:
                     scores(n)
                 if 0 <= n - 1 < BANKS * N_STEP:
                     subtract(n - 1)
-            if starts(s - EXP_LAG, 1):
-                exp_chunk((s - EXP_LAG) // STEPS_U, (s - EXP_LAG) % STEPS_U)
+                if n == BANKS * s:
+                    if starts(s - EXP_LAG, 1):
+                        exp_chunk((s - EXP_LAG) // STEPS_U, (s - EXP_LAG) % STEPS_U)
+                    for x in range(s - SUM_LAG - SUM_WAIT, s - SUM_LAG + 1):
+                        if starts(x, 1) and sum_step(x) == s:
+                            head_sum(x // CHUNKS, x % CHUNKS)
+                    if starts(s - RECIP_LAG, 2 * STEPS_K):
+                        reciprocal((s - RECIP_LAG) // (2 * STEPS_K))
             if starts(s + LOAD_Q_AHEAD, STEPS_QT):
                 b, t, g, j = place(s + LOAD_Q_AHEAD)
                 load_q(b, t)
@@ -283,15 +313,12 @@ def tile_multiheadattention_pa_kernel(tc, query, k, value, out):
                 wt = w_pool.tile([P, H, P, PACK], BF16, align_bytes=64)
                 w[i] = wt
                 weights(i, nc.gpsimd, range(gpsimd_heads(i)))
-            if starts(s - SUM_LAG, 1):
-                head_sum((s - SUM_LAG) // STEPS_U, (s - SUM_LAG) % STEPS_U)
-            if starts(s - RECIP_LAG, 2 * STEPS_K):
-                reciprocal((s - RECIP_LAG) // (2 * STEPS_K))
             if starts(s - VECTOR_SHARE_LAG, STEPS_K):
                 i = (s - VECTOR_SHARE_LAG) // STEPS_K
                 weights(i, nc.vector, range(gpsimd_heads(i), H))
             if starts(s - QUANT_LAG, STEPS_K):
                 quantise((s - QUANT_LAG) // STEPS_K)
-            if starts(s - CONTEXT_LAG - (STEPS_QT - STEPS_K), STEPS_QT):
-                b, t, g, j = place(s - CONTEXT_LAG)
-                context(b, t)
+            for part in range(H // CONTEXT_HEADS):
+                if starts(s - CONTEXT_LAG - part - (STEPS_QT - STEPS_K), STEPS_QT):
+                    b, t, g, j = place(s - CONTEXT_LAG - part)
+                    context(b, t, part)

@@ -44,9 +44,9 @@ BACK_LAG = RECIP_LAG + 4
 VECTOR_SHARE_LAG = BACK_LAG + 4
 QUANT_LAG = BACK_LAG + 6
 CONTEXT_LAG = QUANT_LAG + 4
-CONTEXT_HEADS = 2
+CONTEXT_HEADS = 4
 CHUNKS_PAIR = 2 * HALVES * CHUNKS
-CLOCK_COLS = 256
+CLOCK_COLS = 512
 HEAD_GROUP = 4
 GPSIMD_HEADS = 8
 TAIL_BLOCKS = 4
@@ -283,14 +283,8 @@ def tile_multiheadattention_pa_kernel(tc, query, k, value, out):
                     scores(n)
                 if 0 <= n - 1 < BANKS * N_STEP:
                     subtract(n - 1)
-                if n == BANKS * s:
-                    if starts(s - EXP_LAG, 1):
-                        exp_chunk((s - EXP_LAG) // STEPS_U, (s - EXP_LAG) % STEPS_U)
-                    for x in range(s - SUM_LAG - SUM_WAIT, s - SUM_LAG + 1):
-                        if starts(x, 1) and sum_step(x) == s:
-                            head_sum(x // CHUNKS, x % CHUNKS)
-                    if starts(s - RECIP_LAG, 2 * STEPS_K):
-                        reciprocal((s - RECIP_LAG) // (2 * STEPS_K))
+            if starts(s - EXP_LAG, 1):
+                exp_chunk((s - EXP_LAG) // STEPS_U, (s - EXP_LAG) % STEPS_U)
             if starts(s + LOAD_Q_AHEAD, STEPS_QT):
                 b, t, g, j = place(s + LOAD_Q_AHEAD)
                 load_q(b, t)
@@ -313,6 +307,11 @@ def tile_multiheadattention_pa_kernel(tc, query, k, value, out):
                 wt = w_pool.tile([P, H, P, PACK], BF16, align_bytes=64)
                 w[i] = wt
                 weights(i, nc.gpsimd, range(gpsimd_heads(i)))
+            for x in range(s - SUM_LAG - SUM_WAIT, s - SUM_LAG + 1):
+                if starts(x, 1) and sum_step(x) == s:
+                    head_sum(x // CHUNKS, x % CHUNKS)
+            if starts(s - RECIP_LAG, 2 * STEPS_K):
+                reciprocal((s - RECIP_LAG) // (2 * STEPS_K))
             if starts(s - VECTOR_SHARE_LAG, STEPS_K):
                 i = (s - VECTOR_SHARE_LAG) // STEPS_K
                 weights(i, nc.vector, range(gpsimd_heads(i), H))

@@ -31,44 +31,45 @@ STEPS_B = N_QT * STEPS_QT
 N_STEP = B * STEPS_B
 N_BLOCK = N_STEP // STEPS_K
 
-LOAD_Q_AHEAD = 11
-LOAD_K_AHEAD = 9
+LOAD_Q_AHEAD = 9
+LOAD_K_AHEAD = 3
 PREP_Q_AHEAD = 5
 PREP_K_AHEAD = 5
-PREP_V_LAG = 9
+LOAD_V_STEP = 1
+PREP_V_STEP = 6
 EXP_LAG = STEPS_U
 SUM_LAG = EXP_LAG + 2
 SUM_WAIT = 2
 RECIP_LAG = SUM_LAG + 2 * STEPS_K - 1
-BACK_LAG = RECIP_LAG + 4
-VECTOR_SHARE_LAG = BACK_LAG + 4
-QUANT_LAG = BACK_LAG + 6
-CONTEXT_LAG = QUANT_LAG + 4
+BACK_LAG = RECIP_LAG + 3
+WEIGHT_LAG = BACK_LAG + 1
+QUANT_LAG = WEIGHT_LAG + STEPS_K
+CONTEXT_LAG = QUANT_LAG + 3
 CONTEXT_HEADS = 4
 CHUNKS_PAIR = 2 * HALVES * CHUNKS
 CLOCK_COLS = 512
-HEAD_GROUP = 4
+CLOCK_STEP = PREP_V_STEP + 8
 GPSIMD_HEADS = 8
 TAIL_BLOCKS = 4
-TAIL_GPSIMD_HEADS = 4
+
 
 def tile_multiheadattention_pa_kernel(tc, query, k, value, out):
     nc = tc.nc
     with ExitStack() as ctx:
         ctx.enter_context(tc.manual_schedule())
         const = ctx.enter_context(tc.tile_pool(name="const", bufs=1))
-        kraw_pool = ctx.enter_context(tc.tile_pool(name="kraw", bufs=LOAD_K_AHEAD))
+        kraw_pool = ctx.enter_context(tc.tile_pool(name="kraw", bufs=LOAD_K_AHEAD + 1))
         qraw_pool = ctx.enter_context(tc.tile_pool(name="qraw", bufs=2))
-        kt_pool = ctx.enter_context(tc.tile_pool(name="kt", bufs=N_PASS))
+        kt_pool = ctx.enter_context(tc.tile_pool(name="kt", bufs=2 * N_PASS - 1))
         qt_pool = ctx.enter_context(tc.tile_pool(name="qt", bufs=2))
         v_stage = ctx.enter_context(tc.tile_pool(name="vstage", bufs=1))
         v_keep = ctx.enter_context(tc.tile_pool(name="vkeep", bufs=2))
         shift_pool = ctx.enter_context(tc.tile_pool(name="shift", bufs=3))
-        e_pool = ctx.enter_context(tc.tile_pool(name="e", bufs=10))
+        e_pool = ctx.enter_context(tc.tile_pool(name="e", bufs=9))
         top_pool = ctx.enter_context(tc.tile_pool(name="top", bufs=4))
         r_pool = ctx.enter_context(tc.tile_pool(name="r", bufs=2))
         rs_pool = ctx.enter_context(tc.tile_pool(name="rs", bufs=3))
-        w_pool = ctx.enter_context(tc.tile_pool(name="w", bufs=2))
+        w_pool = ctx.enter_context(tc.tile_pool(name="w", bufs=1))
         code_pool = ctx.enter_context(tc.tile_pool(name="code", bufs=N_PASS + 1))
         o_pool = ctx.enter_context(tc.tile_pool(name="o", bufs=1))
         ps_score = ctx.enter_context(tc.psum_pool(name="ps_score", bufs=4))
@@ -121,7 +122,7 @@ def tile_multiheadattention_pa_kernel(tc, query, k, value, out):
 
         def prep_v(b):
             grouped = v_stage.tile([P, N_PASS, DH, PACK], BF16, align_bytes=64)
-            nc.vector.tensor_copy(out=grouped[:], in_=vraw[b][:].rearrange("p g j d -> p g d j"))
+            nc.gpsimd.tensor_copy(out=grouped[:], in_=vraw[b][:].rearrange("p g j d -> p g d j"))
             vc = v_keep.tile([P, N_PASS * DH], U32, align_bytes=64)
             vs = v_keep.tile([P, N_PASS * DH], U8, align_bytes=64)
             nc.vector.quantize_mx(
@@ -138,13 +139,13 @@ def tile_multiheadattention_pa_kernel(tc, query, k, value, out):
                 st = shift_pool.tile([P, PACK, H, QB], F32)
                 shift[u] = st
             sc = ps_score.tile([P, H * QB], F32)
-            if b in v_codes:
+            if u * STEPS_U >= CLOCK_STEP:
                 nc.tensor.matmul_mx(
                     out=sc[:, :CLOCK_COLS],
-                    lhsT=v_codes[b][:, :P].bitcast(FP8X4),
-                    lhsT_scale=v_scales[b][:, :P],
-                    rhs=v_codes[b][:, :CLOCK_COLS].bitcast(FP8X4),
-                    rhs_scale=v_scales[b][:, :CLOCK_COLS],
+                    lhsT=v_codes[0][:, :P].bitcast(FP8X4),
+                    lhsT_scale=v_scales[0][:, :P],
+                    rhs=v_codes[0][:, :CLOCK_COLS].bitcast(FP8X4),
+                    rhs_scale=v_scales[0][:, :CLOCK_COLS],
                     start=True,
                     stop=True,
                 )
@@ -218,22 +219,21 @@ def tile_multiheadattention_pa_kernel(tc, query, k, value, out):
             r_sb[i] = rs
 
         def gpsimd_heads(i):
-            return GPSIMD_HEADS if i < N_BLOCK - TAIL_BLOCKS else TAIL_GPSIMD_HEADS
+            return GPSIMD_HEADS if i < N_BLOCK - TAIL_BLOCKS else 0
 
         def weights(i, eng, heads):
             for half in range(HALVES):
                 qs = slice(half * QB, (half + 1) * QB)
-                for h in range(heads.start, heads.stop, HEAD_GROUP):
-                    hs = slice(h, h + HEAD_GROUP)
-                    eng.tensor_tensor(
-                        out=w[i][:, hs, qs, :].rearrange("p h q j -> p h (q j)"),
-                        in0=e[i * HALVES + half][:, hs].rearrange("p h q j -> p h (q j)"),
-                        in1=r_sb[i][:, qs, :]
-                        .rearrange("p q j -> p (q j)")
-                        .unsqueeze(1)
-                        .to_broadcast([P, HEAD_GROUP, QB * PACK]),
-                        op=ALU.mult,
-                    )
+                hs = slice(heads.start, heads.stop)
+                eng.tensor_tensor(
+                    out=w[i][:, hs, qs, :].rearrange("p h q j -> p h (q j)"),
+                    in0=e[i * HALVES + half][:, hs].rearrange("p h q j -> p h (q j)"),
+                    in1=r_sb[i][:, qs, :]
+                    .rearrange("p q j -> p (q j)")
+                    .unsqueeze(1)
+                    .to_broadcast([P, len(heads), QB * PACK]),
+                    op=ALU.mult,
+                )
 
         def quantise(i):
             cd = code_pool.tile([P, H * P], U32, align_bytes=64)
@@ -270,6 +270,14 @@ def tile_multiheadattention_pa_kernel(tc, query, k, value, out):
             if CONTEXT_HEADS * (part + 1) == H:
                 nc.sync.dma_start(out=out[b, t * P : (t + 1) * P, :], in_=res[(b, t)][:])
 
+        def piece(r):
+            return r // (N_PASS * PACK), r // PACK % N_PASS, r % PACK
+
+        def prep_step(r):
+            b, g, j = piece(r)
+            x = PACK * g + j
+            return x - PREP_K_AHEAD if b == 0 else (b - 1) * STEPS_B + STEPS_QT + 4 * x
+
         def sum_step(x):
             k = x % CHUNKS_PAIR
             return x - k + SUM_LAG + max(k, SUM_WAIT + k // 2)
@@ -288,35 +296,37 @@ def tile_multiheadattention_pa_kernel(tc, query, k, value, out):
             if starts(s + LOAD_Q_AHEAD, STEPS_QT):
                 b, t, g, j = place(s + LOAD_Q_AHEAD)
                 load_q(b, t)
-                if t == 0:
-                    load_v(b)
-            if starts(s + LOAD_K_AHEAD, 1) and place(s + LOAD_K_AHEAD)[1] == 0:
-                b, t, g, j = place(s + LOAD_K_AHEAD)
-                load_k(b, g, j)
+            for r in range(B * N_PASS * PACK):
+                if s == prep_step(r) - LOAD_K_AHEAD:
+                    load_k(*piece(r))
             if starts(s + PREP_Q_AHEAD, STEPS_QT):
                 b, t, g, j = place(s + PREP_Q_AHEAD)
                 prep_q(b, t)
-            if starts(s + PREP_K_AHEAD, 1) and place(s + PREP_K_AHEAD)[1] == 0:
-                b, t, g, j = place(s + PREP_K_AHEAD)
-                prep_k(b, g, j)
-            if starts(s - PREP_V_LAG, STEPS_B):
-                prep_v((s - PREP_V_LAG) // STEPS_B)
+            for r in range(B * N_PASS * PACK):
+                if s == prep_step(r):
+                    prep_k(*piece(r))
+            if s - LOAD_V_STEP in range(B):
+                load_v(s - LOAD_V_STEP)
+            if s - PREP_V_STEP in range(B):
+                prep_v(s - PREP_V_STEP)
             if starts(s - BACK_LAG, STEPS_K):
                 i = (s - BACK_LAG) // STEPS_K
                 reciprocal_back(i)
-                wt = w_pool.tile([P, H, P, PACK], BF16, align_bytes=64)
-                w[i] = wt
-                weights(i, nc.gpsimd, range(gpsimd_heads(i)))
             for x in range(s - SUM_LAG - SUM_WAIT, s - SUM_LAG + 1):
                 if starts(x, 1) and sum_step(x) == s:
                     head_sum(x // CHUNKS, x % CHUNKS)
             if starts(s - RECIP_LAG, 2 * STEPS_K):
                 reciprocal((s - RECIP_LAG) // (2 * STEPS_K))
-            if starts(s - VECTOR_SHARE_LAG, STEPS_K):
-                i = (s - VECTOR_SHARE_LAG) // STEPS_K
-                weights(i, nc.vector, range(gpsimd_heads(i), H))
             if starts(s - QUANT_LAG, STEPS_K):
                 quantise((s - QUANT_LAG) // STEPS_K)
+            if starts(s - WEIGHT_LAG, STEPS_K):
+                i = (s - WEIGHT_LAG) // STEPS_K
+                wt = w_pool.tile([P, H, P, PACK], BF16, align_bytes=64)
+                w[i] = wt
+                if gpsimd_heads(i) < H:
+                    weights(i, nc.vector, range(gpsimd_heads(i), H))
+                if gpsimd_heads(i) > 0:
+                    weights(i, nc.gpsimd, range(gpsimd_heads(i)))
             for part in range(H // CONTEXT_HEADS):
                 if starts(s - CONTEXT_LAG - part - (STEPS_QT - STEPS_K), STEPS_QT):
                     b, t, g, j = place(s - CONTEXT_LAG - part)

@@ -45,10 +45,12 @@ BACK_LAG = RECIP_LAG + 3
 WEIGHT_LAG = BACK_LAG + 1
 QUANT_LAG = WEIGHT_LAG + STEPS_K
 CONTEXT_LAG = QUANT_LAG + 3
+LAST_SUM_STEP = N_STEP + SUM_LAG - 1 + 1
 CONTEXT_HEADS = 4
 CHUNKS_PAIR = 2 * HALVES * CHUNKS
 CLOCK_COLS = 512
 CLOCK_STEP = PREP_V_STEP + 8
+WARM_BANKS = 28
 GPSIMD_HEADS = 8
 TAIL_BLOCKS = 4
 
@@ -81,6 +83,9 @@ def tile_multiheadattention_pa_kernel(tc, query, k, value, out):
         ident_f = const.tile([P, P], F32)
         make_identity(nc, ident_f[:])
 
+        zeros = const.tile([P, H * QB], BF16)
+        nc.vector.memset(zeros[:], 0.0)
+
         kraw, qraw, vraw, k_t, q_t, v_codes, v_scales = {}, {}, {}, {}, {}, {}, {}
         bank, shift, e, sum_t, r_t, r_sb, w, codes, scales, acc, res = {}, {}, {}, {}, {}, {}, {}, {}, {}, {}, {}
 
@@ -102,6 +107,10 @@ def tile_multiheadattention_pa_kernel(tc, query, k, value, out):
             raw = v_stage.tile([P, N_PASS, PACK, DH], BF16)
             nc.sync.dma_start(out=raw[:], in_=value[b].rearrange("(g p j) d -> p g j d", p=P, j=PACK))
             vraw[b] = raw
+
+        def warm_up():
+            sc = ps_score.tile([P, H * QB], F32, tag="score")
+            warm(sc)
 
         def transpose_heads(raw, dst):
             tp = ps_misc.tile([P, H, P], BF16, tag="misc")
@@ -131,6 +140,9 @@ def tile_multiheadattention_pa_kernel(tc, query, k, value, out):
             v_codes[b] = vc
             v_scales[b] = vs
 
+        def warm(dst, cols=H * QB):
+            nc.tensor.matmul(out=dst[:, :cols], lhsT=zeros[:, :P], rhs=zeros[:, :cols], start=True, stop=True)
+
         def scores(n):
             u, j = n // PACK, n % PACK
             half = u % HALVES
@@ -138,8 +150,10 @@ def tile_multiheadattention_pa_kernel(tc, query, k, value, out):
             if j == 0:
                 st = shift_pool.tile([P, PACK, H, QB], F32)
                 shift[u] = st
-            sc = ps_score.tile([P, H * QB], F32)
-            if u * STEPS_U >= CLOCK_STEP:
+            sc = ps_score.tile([P, H * QB], F32, tag="score")
+            if n < WARM_BANKS:
+                warm(sc, 256)
+            elif u * STEPS_U >= CLOCK_STEP:
                 nc.tensor.matmul_mx(
                     out=sc[:, :CLOCK_COLS],
                     lhsT=v_codes[0][:, :P].bitcast(FP8X4),
@@ -276,7 +290,11 @@ def tile_multiheadattention_pa_kernel(tc, query, k, value, out):
         def prep_step(r):
             b, g, j = piece(r)
             x = PACK * g + j
-            return x - PREP_K_AHEAD if b == 0 else (b - 1) * STEPS_B + STEPS_QT + 4 * x
+            return x - PREP_K_AHEAD if b == 0 else (b - 1) * STEPS_B + STEPS_QT - STEPS_K + 4 * x
+
+        def weight_step(i):
+            due = STEPS_K * i + WEIGHT_LAG
+            return max(due, N_STEP + 1) if i >= N_BLOCK - TAIL_BLOCKS else due
 
         def sum_step(x):
             k = x % CHUNKS_PAIR
@@ -299,6 +317,12 @@ def tile_multiheadattention_pa_kernel(tc, query, k, value, out):
             for r in range(B * N_PASS * PACK):
                 if s == prep_step(r) - LOAD_K_AHEAD:
                     load_k(*piece(r))
+            if s == -PREP_Q_AHEAD:
+                for n0 in range(4):
+                    warm_up()
+            elif -PREP_Q_AHEAD < s < 0:
+                for n0 in range(1):
+                    warm_up()
             if starts(s + PREP_Q_AHEAD, STEPS_QT):
                 b, t, g, j = place(s + PREP_Q_AHEAD)
                 prep_q(b, t)
@@ -319,8 +343,9 @@ def tile_multiheadattention_pa_kernel(tc, query, k, value, out):
                 reciprocal((s - RECIP_LAG) // (2 * STEPS_K))
             if starts(s - QUANT_LAG, STEPS_K):
                 quantise((s - QUANT_LAG) // STEPS_K)
-            if starts(s - WEIGHT_LAG, STEPS_K):
-                i = (s - WEIGHT_LAG) // STEPS_K
+            for i in range(N_BLOCK):
+                if s != weight_step(i):
+                    continue
                 wt = w_pool.tile([P, H, P, PACK], BF16, align_bytes=64)
                 w[i] = wt
                 if gpsimd_heads(i) < H:
@@ -328,6 +353,7 @@ def tile_multiheadattention_pa_kernel(tc, query, k, value, out):
                 if gpsimd_heads(i) > 0:
                     weights(i, nc.gpsimd, range(gpsimd_heads(i)))
             for part in range(H // CONTEXT_HEADS):
-                if starts(s - CONTEXT_LAG - part - (STEPS_QT - STEPS_K), STEPS_QT):
-                    b, t, g, j = place(s - CONTEXT_LAG - part)
-                    context(b, t, part)
+                for q in range(B * N_QT):
+                    due = STEPS_QT * (q + 1) - STEPS_K + CONTEXT_LAG
+                    if s == part + (max(due, LAST_SUM_STEP + 1) if due > N_STEP else due):
+                        context(q // N_QT, q % N_QT, part)

@@ -43,8 +43,8 @@ SUM_WAIT = 2
 RECIP_LAG = SUM_LAG + 2 * STEPS_K - 1
 BACK_LAG = RECIP_LAG + 3
 WEIGHT_LAG = BACK_LAG + 1
-QUANT_LAG = WEIGHT_LAG + STEPS_K
-CONTEXT_LAG = QUANT_LAG + 3
+QUANT_LAG = WEIGHT_LAG + 2 * STEPS_K
+CONTEXT_LAG = QUANT_LAG - STEPS_K + 3
 LAST_SUM_STEP = N_STEP + SUM_LAG - 1 + 1
 CONTEXT_HEADS = 4
 CHUNKS_PAIR = 2 * HALVES * CHUNKS
@@ -61,7 +61,7 @@ def tile_multiheadattention_pa_kernel(tc, query, k, value, out):
         ctx.enter_context(tc.manual_schedule())
         const = ctx.enter_context(tc.tile_pool(name="const", bufs=1))
         kraw_pool = ctx.enter_context(tc.tile_pool(name="kraw", bufs=LOAD_K_AHEAD + 1))
-        qraw_pool = ctx.enter_context(tc.tile_pool(name="qraw", bufs=2))
+        qraw_pool = ctx.enter_context(tc.tile_pool(name="qraw", bufs=1))
         kt_pool = ctx.enter_context(tc.tile_pool(name="kt", bufs=2 * N_PASS - 1))
         qt_pool = ctx.enter_context(tc.tile_pool(name="qt", bufs=2))
         v_stage = ctx.enter_context(tc.tile_pool(name="vstage", bufs=1))
@@ -70,8 +70,8 @@ def tile_multiheadattention_pa_kernel(tc, query, k, value, out):
         e_pool = ctx.enter_context(tc.tile_pool(name="e", bufs=9))
         top_pool = ctx.enter_context(tc.tile_pool(name="top", bufs=4))
         r_pool = ctx.enter_context(tc.tile_pool(name="r", bufs=2))
-        rs_pool = ctx.enter_context(tc.tile_pool(name="rs", bufs=3))
-        w_pool = ctx.enter_context(tc.tile_pool(name="w", bufs=1))
+        rs_pool = ctx.enter_context(tc.tile_pool(name="rs", bufs=2))
+        w_pool = ctx.enter_context(tc.tile_pool(name="w", bufs=2))
         code_pool = ctx.enter_context(tc.tile_pool(name="code", bufs=N_PASS + 1))
         o_pool = ctx.enter_context(tc.tile_pool(name="o", bufs=1))
         ps_score = ctx.enter_context(tc.psum_pool(name="ps_score", bufs=4))
@@ -296,6 +296,10 @@ def tile_multiheadattention_pa_kernel(tc, query, k, value, out):
             due = STEPS_K * i + WEIGHT_LAG
             return max(due, N_STEP + 1) if i >= N_BLOCK - TAIL_BLOCKS else due
 
+        def quant_step(m):
+            due = 2 * STEPS_K * m + QUANT_LAG
+            return due
+
         def sum_step(x):
             k = x % CHUNKS_PAIR
             return x - k + SUM_LAG + max(k, SUM_WAIT + k // 2)
@@ -341,8 +345,10 @@ def tile_multiheadattention_pa_kernel(tc, query, k, value, out):
                     head_sum(x // CHUNKS, x % CHUNKS)
             if starts(s - RECIP_LAG, 2 * STEPS_K):
                 reciprocal((s - RECIP_LAG) // (2 * STEPS_K))
-            if starts(s - QUANT_LAG, STEPS_K):
-                quantise((s - QUANT_LAG) // STEPS_K)
+            for m in range(N_BLOCK // 2):
+                if s == quant_step(m):
+                    quantise(2 * m)
+                    quantise(2 * m + 1)
             for i in range(N_BLOCK):
                 if s != weight_step(i):
                     continue

@@ -22,6 +22,7 @@ N_QT = TQ // P
 QB = 64
 QC = P // PACK
 HALVES = P // QB
+RUN = 4
 CHUNKS = QB // QC
 BANKS = 2
 STEPS_U = PACK // BANKS
@@ -148,7 +149,7 @@ def tile_multiheadattention_pa_kernel(tc, query, k, value, out):
             half = u % HALVES
             b, t, g, first = place(u * STEPS_U)
             if j == 0:
-                st = shift_pool.tile([P, PACK, H, QB], F32)
+                st = shift_pool.tile([P, CHUNKS, PACK, H, QC], F32)
                 shift[u] = st
             sc = ps_score.tile([P, H * QB], F32, tag="score")
             if n < WARM_BANKS:
@@ -180,20 +181,19 @@ def tile_multiheadattention_pa_kernel(tc, query, k, value, out):
         def subtract(n):
             sc, top = bank[n]
             nc.vector.tensor_tensor(
-                out=shift[n // PACK][:, n % PACK],
-                in0=sc[:].rearrange("p (h q) -> p h q", h=H),
-                in1=top[:].unsqueeze(1).to_broadcast([P, H, QB]),
+                out=shift[n // PACK][:, :, n % PACK],
+                in0=sc[:].rearrange("p (h c q) -> p c h q", h=H, c=CHUNKS),
+                in1=top[:].rearrange("p (c q) -> p c q", c=CHUNKS).unsqueeze(2).to_broadcast([P, CHUNKS, H, QC]),
                 op=ALU.subtract,
             )
 
         def exp_chunk(u, c):
             if c == 0:
-                et = e_pool.tile([P, H, QB, PACK], F32)
+                et = e_pool.tile([P, CHUNKS, H, QC, PACK], F32)
                 e[u] = et
-            cols = slice(c * QC, (c + 1) * QC)
             nc.scalar.activation(
-                out=e[u][:, :, cols, :],
-                in_=shift[u][:, :, :, cols].rearrange("p j h q -> p h q j"),
+                out=e[u][:, c].rearrange("p h (a n) j -> p (h a) j n", n=RUN),
+                in_=shift[u][:, c].rearrange("p j h (a n) -> p (h a) j n", n=RUN),
                 func=ACT.Exp,
                 scale=DH**-0.5,
             )
@@ -207,7 +207,7 @@ def tile_multiheadattention_pa_kernel(tc, query, k, value, out):
             for h in range(H):
                 nc.tensor.matmul(
                     out=sum_t[i][:, col : col + P],
-                    lhsT=e[u][:, h, c * QC : (c + 1) * QC, :].rearrange("p q j -> p (q j)"),
+                    lhsT=e[u][:, c, h].rearrange("p q j -> p (q j)"),
                     rhs=ident_f[:],
                     is_transpose=True,
                     start=(h == 0),
@@ -237,26 +237,33 @@ def tile_multiheadattention_pa_kernel(tc, query, k, value, out):
 
         def weights(i, eng, heads):
             for half in range(HALVES):
-                qs = slice(half * QB, (half + 1) * QB)
+                cols = slice(half * QB * PACK, (half + 1) * QB * PACK)
                 hs = slice(heads.start, heads.stop)
                 eng.tensor_tensor(
-                    out=w[i][:, hs, qs, :].rearrange("p h q j -> p h (q j)"),
-                    in0=e[i * HALVES + half][:, hs].rearrange("p h q j -> p h (q j)"),
-                    in1=r_sb[i][:, qs, :]
-                    .rearrange("p q j -> p (q j)")
-                    .unsqueeze(1)
-                    .to_broadcast([P, len(heads), QB * PACK]),
+                    out=w[i][:, hs].rearrange("p h q j -> p h (q j)")[:, :, cols].rearrange(
+                        "p h (c x) -> p c h x", c=CHUNKS
+                    ),
+                    in0=e[i * HALVES + half][:, :, hs].rearrange("p c h q j -> p c h (q j)"),
+                    in1=r_sb[i][:]
+                    .rearrange("p q j -> p (q j)")[:, cols]
+                    .rearrange("p (c x) -> p c x", c=CHUNKS)
+                    .unsqueeze(2)
+                    .to_broadcast([P, CHUNKS, len(heads), QC * PACK]),
                     op=ALU.mult,
                 )
 
-        def quantise(i):
-            cd = code_pool.tile([P, H * P], U32, align_bytes=64)
-            sl = code_pool.tile([P, H * P], U8, align_bytes=64)
+        def quantise(i, heads=range(H)):
+            if heads.start == 0:
+                cd = code_pool.tile([P, H * P], U32, align_bytes=64)
+                sl = code_pool.tile([P, H * P], U8, align_bytes=64)
+                codes[i] = cd
+                scales[i] = sl
+            cols = slice(heads.start * P, heads.stop * P)
             nc.vector.quantize_mx(
-                out=cd[:].bitcast(FP8X4), scales=sl[:], in_=w[i][:].rearrange("p h q j -> p (h q j)")
+                out=codes[i][:, cols].bitcast(FP8X4),
+                scales=scales[i][:, cols],
+                in_=w[i][:, heads.start : heads.stop].rearrange("p h q j -> p (h q j)"),
             )
-            codes[i] = cd
-            scales[i] = sl
 
         def context(b, t, part):
             per_bank = 4
@@ -279,10 +286,9 @@ def tile_multiheadattention_pa_kernel(tc, query, k, value, out):
                         stop=(g == N_PASS - 1),
                     )
                 if h % per_bank == per_bank - 1:
-                    first = (h - per_bank + 1) * DH
-                    nc.scalar.copy(out=res[(b, t)][:, first : (h + 1) * DH], in_=acc[(b, t)][:])
-            if CONTEXT_HEADS * (part + 1) == H:
-                nc.sync.dma_start(out=out[b, t * P : (t + 1) * P, :], in_=res[(b, t)][:])
+                    cols = slice((h - per_bank + 1) * DH, (h + 1) * DH)
+                    nc.scalar.copy(out=res[(b, t)][:, cols], in_=acc[(b, t)][:])
+                    nc.sync.dma_start(out=out[b, t * P : (t + 1) * P, cols], in_=res[(b, t)][:, cols])
 
         def piece(r):
             return r // (N_PASS * PACK), r // PACK % N_PASS, r % PACK
@@ -348,14 +354,19 @@ def tile_multiheadattention_pa_kernel(tc, query, k, value, out):
             for m in range(N_BLOCK // 2):
                 if s == quant_step(m):
                     quantise(2 * m)
-                    quantise(2 * m + 1)
+                    if m < N_BLOCK // 2 - 1:
+                        quantise(2 * m + 1)
+                    else:
+                        quantise(2 * m + 1, range(H // 2))
+                        weights(2 * m + 1, nc.vector, range(H // 2, H))
+                        quantise(2 * m + 1, range(H // 2, H))
             for i in range(N_BLOCK):
                 if s != weight_step(i):
                     continue
                 wt = w_pool.tile([P, H, P, PACK], BF16, align_bytes=64)
                 w[i] = wt
                 if gpsimd_heads(i) < H:
-                    weights(i, nc.vector, range(gpsimd_heads(i), H))
+                    weights(i, nc.vector, range(H // 2 if i == N_BLOCK - 1 else H))
                 if gpsimd_heads(i) > 0:
                     weights(i, nc.gpsimd, range(gpsimd_heads(i)))
             for part in range(H // CONTEXT_HEADS):

@@ -49,7 +49,7 @@ CONTEXT_LAG = QUANT_LAG - STEPS_K + 3
 LAST_SUM_STEP = N_STEP + SUM_LAG - 1 + 1
 CONTEXT_HEADS = 4
 CHUNKS_PAIR = 2 * HALVES * CHUNKS
-CLOCK_COLS = 512
+CLOCK_COLS = 256
 CLOCK_STEP = PREP_V_STEP + 8
 WARM_BANKS = 28
 GPSIMD_HEADS = 8

from contextlib import ExitStack

import concourse.mybir as mybir
from concourse.masks import make_identity

B, TQ, TV, H, DH = 2, 512, 2048, 8, 128
FLOPS = 2 * 2 * B * H * TQ * TV * DH

F32 = mybir.dt.float32
BF16 = mybir.dt.bfloat16
U32 = mybir.dt.uint32
U8 = mybir.dt.uint8
FP8X4 = mybir.dt.float8_e4m3fn_x4
ALU = mybir.AluOpType
ACT = mybir.ActivationFunctionType

P = 128
PACK = 4
K_PASS = P * PACK
N_PASS = TV // K_PASS
N_QT = TQ // P
QB = 64
QC = P // PACK
HALVES = P // QB
RUN = 4
CHUNKS = QB // QC
BANKS = 2
STEPS_U = PACK // BANKS
STEPS_K = HALVES * STEPS_U
STEPS_QT = N_PASS * STEPS_K
STEPS_B = N_QT * STEPS_QT
N_STEP = B * STEPS_B
N_BLOCK = N_STEP // STEPS_K

LOAD_Q_AHEAD = 9
LOAD_K_AHEAD = 3
PREP_Q_AHEAD = 5
PREP_K_AHEAD = 5
LOAD_V_STEP = 1
PREP_V_STEP = 6
EXP_LAG = STEPS_U
SUM_LAG = EXP_LAG + 2
SUM_WAIT = 2
RECIP_LAG = SUM_LAG + 2 * STEPS_K - 1
BACK_LAG = RECIP_LAG + 3
WEIGHT_LAG = BACK_LAG + 1
QUANT_LAG = WEIGHT_LAG + 2 * STEPS_K
CONTEXT_LAG = QUANT_LAG - STEPS_K + 3
LAST_SUM_STEP = N_STEP + SUM_LAG - 1 + 1
CONTEXT_HEADS = 4
CHUNKS_PAIR = 2 * HALVES * CHUNKS
CLOCK_COLS = 256
CLOCK_STEP = PREP_V_STEP + 8
WARM_BANKS = 28
GPSIMD_HEADS = 8
TAIL_BLOCKS = 4


def tile_multiheadattention_pa_kernel(tc, query, k, value, out):
    nc = tc.nc
    with ExitStack() as ctx:
        ctx.enter_context(tc.manual_schedule())
        const = ctx.enter_context(tc.tile_pool(name="const", bufs=1))
        kraw_pool = ctx.enter_context(tc.tile_pool(name="kraw", bufs=LOAD_K_AHEAD + 1))
        qraw_pool = ctx.enter_context(tc.tile_pool(name="qraw", bufs=1))
        kt_pool = ctx.enter_context(tc.tile_pool(name="kt", bufs=2 * N_PASS - 1))
        qt_pool = ctx.enter_context(tc.tile_pool(name="qt", bufs=2))
        v_stage = ctx.enter_context(tc.tile_pool(name="vstage", bufs=1))
        v_keep = ctx.enter_context(tc.tile_pool(name="vkeep", bufs=2))
        shift_pool = ctx.enter_context(tc.tile_pool(name="shift", bufs=3))
        e_pool = ctx.enter_context(tc.tile_pool(name="e", bufs=9))
        top_pool = ctx.enter_context(tc.tile_pool(name="top", bufs=4))
        r_pool = ctx.enter_context(tc.tile_pool(name="r", bufs=2))
        rs_pool = ctx.enter_context(tc.tile_pool(name="rs", bufs=2))
        w_pool = ctx.enter_context(tc.tile_pool(name="w", bufs=2))
        code_pool = ctx.enter_context(tc.tile_pool(name="code", bufs=N_PASS + 1))
        o_pool = ctx.enter_context(tc.tile_pool(name="o", bufs=1))
        ps_score = ctx.enter_context(tc.psum_pool(name="ps_score", bufs=4))
        ps_sum = ctx.enter_context(tc.psum_pool(name="ps_sum", bufs=2))
        ps_misc = ctx.enter_context(tc.psum_pool(name="ps_misc", bufs=2))

        ident_bf = const.tile([P, P], BF16)
        make_identity(nc, ident_bf[:])
        ident_f = const.tile([P, P], F32)
        make_identity(nc, ident_f[:])

        zeros = const.tile([P, H * QB], BF16)
        nc.vector.memset(zeros[:], 0.0)

        kraw, qraw, vraw, k_t, q_t, v_codes, v_scales = {}, {}, {}, {}, {}, {}, {}
        bank, shift, e, sum_t, r_t, r_sb, w, codes, scales, acc, res = {}, {}, {}, {}, {}, {}, {}, {}, {}, {}, {}

        def place(s):
            return s // STEPS_B, (s % STEPS_B) // STEPS_QT, (s % STEPS_QT) // STEPS_K, s % STEPS_K

        def load_q(b, t):
            raw = qraw_pool.tile([P, H * DH], BF16)
            nc.sync.dma_start(out=raw[:], in_=query[b, t * P : (t + 1) * P, :])
            qraw[(b, t)] = raw

        def load_k(b, g, j):
            raw = kraw_pool.tile([P, H * DH], BF16)
            rows = k[b, g * K_PASS : (g + 1) * K_PASS, :].rearrange("(p j) c -> p j c", j=PACK)
            nc.sync.dma_start(out=raw[:], in_=rows[:, j, :])
            kraw[(b, g, j)] = raw

        def load_v(b):
            raw = v_stage.tile([P, N_PASS, PACK, DH], BF16)
            nc.sync.dma_start(out=raw[:], in_=value[b].rearrange("(g p j) d -> p g j d", p=P, j=PACK))
            vraw[b] = raw

        def warm_up():
            sc = ps_score.tile([P, H * QB], F32, tag="score")
            warm(sc)

        def transpose_heads(raw, dst):
            tp = ps_misc.tile([P, H, P], BF16, tag="misc")
            for h in range(H):
                nc.tensor.transpose(out=tp[:, h, :], in_=raw[:, h * DH : (h + 1) * DH], identity=ident_bf[:])
            nc.scalar.copy(out=dst, in_=tp[:])

        def prep_q(b, t):
            qt = qt_pool.tile([P, H, P], BF16)
            transpose_heads(qraw[(b, t)], qt[:])
            q_t[(b, t)] = qt

        def prep_k(b, g, j):
            if j == 0:
                kt = kt_pool.tile([P, PACK, H, P], BF16)
                k_t[(b, g)] = kt
            transpose_heads(kraw[(b, g, j)], k_t[(b, g)][:, j])

        def prep_v(b):
            grouped = v_stage.tile([P, N_PASS, DH, PACK], BF16, align_bytes=64)
            nc.gpsimd.tensor_copy(out=grouped[:], in_=vraw[b][:].rearrange("p g j d -> p g d j"))
            vc = v_keep.tile([P, N_PASS * DH], U32, align_bytes=64)
            vs = v_keep.tile([P, N_PASS * DH], U8, align_bytes=64)
            nc.vector.quantize_mx(
                out=vc[:].bitcast(FP8X4), scales=vs[:], in_=grouped[:].rearrange("p g d j -> p (g d j)")
            )
            v_codes[b] = vc
            v_scales[b] = vs

        def warm(dst, cols=H * QB):
            nc.tensor.matmul(out=dst[:, :cols], lhsT=zeros[:, :P], rhs=zeros[:, :cols], start=True, stop=True)

        def scores(n):
            u, j = n // PACK, n % PACK
            half = u % HALVES
            b, t, g, first = place(u * STEPS_U)
            if j == 0:
                st = shift_pool.tile([P, CHUNKS, PACK, H, QC], F32)
                shift[u] = st
            sc = ps_score.tile([P, H * QB], F32, tag="score")
            if n < WARM_BANKS:
                warm(sc, 256)
            elif u * STEPS_U >= CLOCK_STEP:
                nc.tensor.matmul_mx(
                    out=sc[:, :CLOCK_COLS],
                    lhsT=v_codes[0][:, :P].bitcast(FP8X4),
                    lhsT_scale=v_scales[0][:, :P],
                    rhs=v_codes[0][:, :CLOCK_COLS].bitcast(FP8X4),
                    rhs_scale=v_scales[0][:, :CLOCK_COLS],
                    start=True,
                    stop=True,
                )
            for h in range(H):
                nc.tensor.matmul(
                    out=sc[:, h * QB : (h + 1) * QB],
                    lhsT=k_t[(b, g)][:, j, h, :],
                    rhs=q_t[(b, t)][:, h, half * QB : (half + 1) * QB],
                    start=True,
                    stop=True,
                )
            top = top_pool.tile([P, QB], F32)
            nc.vector.tensor_reduce(
                out=top[:], in_=sc[:].rearrange("p (h q) -> p q h", h=H), axis=mybir.AxisListType.X, op=ALU.max
            )
            bank[n] = (sc, top)

        def subtract(n):
            sc, top = bank[n]
            nc.vector.tensor_tensor(
                out=shift[n // PACK][:, :, n % PACK],
                in0=sc[:].rearrange("p (h c q) -> p c h q", h=H, c=CHUNKS),
                in1=top[:].rearrange("p (c q) -> p c q", c=CHUNKS).unsqueeze(2).to_broadcast([P, CHUNKS, H, QC]),
                op=ALU.subtract,
            )

        def exp_chunk(u, c):
            if c == 0:
                et = e_pool.tile([P, CHUNKS, H, QC, PACK], F32)
                e[u] = et
            nc.scalar.activation(
                out=e[u][:, c].rearrange("p h (a n) j -> p (h a) j n", n=RUN),
                in_=shift[u][:, c].rearrange("p j h (a n) -> p (h a) j n", n=RUN),
                func=ACT.Exp,
                scale=DH**-0.5,
            )

        def head_sum(u, c):
            i, half = u // HALVES, u % HALVES
            if half == 0 and c == 0:
                st = ps_sum.tile([P, PACK * P], F32)
                sum_t[i] = st
            col = (half * CHUNKS + c) * P
            for h in range(H):
                nc.tensor.matmul(
                    out=sum_t[i][:, col : col + P],
                    lhsT=e[u][:, c, h].rearrange("p q j -> p (q j)"),
                    rhs=ident_f[:],
                    is_transpose=True,
                    start=(h == 0),
                    stop=(h == H - 1),
                )

        def reciprocal(m):
            rt = r_pool.tile([P, 2, PACK * P], F32)
            for n in range(2):
                nc.scalar.activation(out=rt[:, n], in_=sum_t[2 * m + n][:], func=ACT.Ln)
            r_t[m] = rt

        def reciprocal_back(i):
            rp = ps_misc.tile([P, PACK * P], F32, tag="misc")
            for col in range(0, PACK * P, P):
                nc.tensor.transpose(
                    out=rp[:, col : col + P], in_=r_t[i // 2][:, i % 2, col : col + P], identity=ident_f[:]
                )
            rs = rs_pool.tile([P, P, PACK], F32)
            nc.scalar.activation(
                out=rs[:].rearrange("p q j -> p (q j)"), in_=rp[:], func=ACT.Exp, scale=-1.0
            )
            r_sb[i] = rs

        def gpsimd_heads(i):
            return GPSIMD_HEADS if i < N_BLOCK - TAIL_BLOCKS else 0

        def weights(i, eng, heads):
            for half in range(HALVES):
                cols = slice(half * QB * PACK, (half + 1) * QB * PACK)
                hs = slice(heads.start, heads.stop)
                eng.tensor_tensor(
                    out=w[i][:, hs].rearrange("p h q j -> p h (q j)")[:, :, cols].rearrange(
                        "p h (c x) -> p c h x", c=CHUNKS
                    ),
                    in0=e[i * HALVES + half][:, :, hs].rearrange("p c h q j -> p c h (q j)"),
                    in1=r_sb[i][:]
                    .rearrange("p q j -> p (q j)")[:, cols]
                    .rearrange("p (c x) -> p c x", c=CHUNKS)
                    .unsqueeze(2)
                    .to_broadcast([P, CHUNKS, len(heads), QC * PACK]),
                    op=ALU.mult,
                )

        def quantise(i, heads=range(H)):
            if heads.start == 0:
                cd = code_pool.tile([P, H * P], U32, align_bytes=64)
                sl = code_pool.tile([P, H * P], U8, align_bytes=64)
                codes[i] = cd
                scales[i] = sl
            cols = slice(heads.start * P, heads.stop * P)
            nc.vector.quantize_mx(
                out=codes[i][:, cols].bitcast(FP8X4),
                scales=scales[i][:, cols],
                in_=w[i][:, heads.start : heads.stop].rearrange("p h q j -> p (h q j)"),
            )

        def context(b, t, part):
            per_bank = 4
            if part == 0:
                rt = o_pool.tile([P, H * DH], F32)
                res[(b, t)] = rt
            for h in range(CONTEXT_HEADS * part, CONTEXT_HEADS * (part + 1)):
                if h % per_bank == 0:
                    at = ps_misc.tile([P, per_bank * DH], F32, tag="misc")
                    acc[(b, t)] = at
                for g in range(N_PASS):
                    i = (b * N_QT + t) * N_PASS + g
                    nc.tensor.matmul_mx(
                        out=acc[(b, t)][:, h % per_bank * DH : (h % per_bank + 1) * DH],
                        lhsT=codes[i][:, h * P : (h + 1) * P].bitcast(FP8X4),
                        lhsT_scale=scales[i][:, h * P : (h + 1) * P],
                        rhs=v_codes[b][:, g * DH : (g + 1) * DH].bitcast(FP8X4),
                        rhs_scale=v_scales[b][:, g * DH : (g + 1) * DH],
                        start=(g == 0),
                        stop=(g == N_PASS - 1),
                    )
                if h % per_bank == per_bank - 1:
                    cols = slice((h - per_bank + 1) * DH, (h + 1) * DH)
                    nc.scalar.copy(out=res[(b, t)][:, cols], in_=acc[(b, t)][:])
                    nc.sync.dma_start(out=out[b, t * P : (t + 1) * P, cols], in_=res[(b, t)][:, cols])

        def piece(r):
            return r // (N_PASS * PACK), r // PACK % N_PASS, r % PACK

        def prep_step(r):
            b, g, j = piece(r)
            x = PACK * g + j
            return x - PREP_K_AHEAD if b == 0 else (b - 1) * STEPS_B + STEPS_QT - STEPS_K + 4 * x

        def weight_step(i):
            due = STEPS_K * i + WEIGHT_LAG
            return max(due, N_STEP + 1) if i >= N_BLOCK - TAIL_BLOCKS else due

        def quant_step(m):
            due = 2 * STEPS_K * m + QUANT_LAG
            return due

        def sum_step(x):
            k = x % CHUNKS_PAIR
            return x - k + SUM_LAG + max(k, SUM_WAIT + k // 2)

        def starts(s, period):
            return 0 <= s < N_STEP and s % period == 0

        for s in range(-LOAD_Q_AHEAD, N_STEP + CONTEXT_LAG + H // CONTEXT_HEADS):
            for n in range(BANKS * s, BANKS * (s + 1)):
                if 0 <= n < BANKS * N_STEP:
                    scores(n)
                if 0 <= n - 1 < BANKS * N_STEP:
                    subtract(n - 1)
            if starts(s - EXP_LAG, 1):
                exp_chunk((s - EXP_LAG) // STEPS_U, (s - EXP_LAG) % STEPS_U)
            if starts(s + LOAD_Q_AHEAD, STEPS_QT):
                b, t, g, j = place(s + LOAD_Q_AHEAD)
                load_q(b, t)
            for r in range(B * N_PASS * PACK):
                if s == prep_step(r) - LOAD_K_AHEAD:
                    load_k(*piece(r))
            if s == -PREP_Q_AHEAD:
                for n0 in range(4):
                    warm_up()
            elif -PREP_Q_AHEAD < s < 0:
                for n0 in range(1):
                    warm_up()
            if starts(s + PREP_Q_AHEAD, STEPS_QT):
                b, t, g, j = place(s + PREP_Q_AHEAD)
                prep_q(b, t)
            for r in range(B * N_PASS * PACK):
                if s == prep_step(r):
                    prep_k(*piece(r))
            if s - LOAD_V_STEP in range(B):
                load_v(s - LOAD_V_STEP)
            if s - PREP_V_STEP in range(B):
                prep_v(s - PREP_V_STEP)
            if starts(s - BACK_LAG, STEPS_K):
                i = (s - BACK_LAG) // STEPS_K
                reciprocal_back(i)
            for x in range(s - SUM_LAG - SUM_WAIT, s - SUM_LAG + 1):
                if starts(x, 1) and sum_step(x) == s:
                    head_sum(x // CHUNKS, x % CHUNKS)
            if starts(s - RECIP_LAG, 2 * STEPS_K):
                reciprocal((s - RECIP_LAG) // (2 * STEPS_K))
            for m in range(N_BLOCK // 2):
                if s == quant_step(m):
                    quantise(2 * m)
                    if m < N_BLOCK // 2 - 1:
                        quantise(2 * m + 1)
                    else:
                        quantise(2 * m + 1, range(H // 2))
                        weights(2 * m + 1, nc.vector, range(H // 2, H))
                        quantise(2 * m + 1, range(H // 2, H))
            for i in range(N_BLOCK):
                if s != weight_step(i):
                    continue
                wt = w_pool.tile([P, H, P, PACK], BF16, align_bytes=64)
                w[i] = wt
                if gpsimd_heads(i) < H:
                    weights(i, nc.vector, range(H // 2 if i == N_BLOCK - 1 else H))
                if gpsimd_heads(i) > 0:
                    weights(i, nc.gpsimd, range(gpsimd_heads(i)))
            for part in range(H // CONTEXT_HEADS):
                for q in range(B * N_QT):
                    due = STEPS_QT * (q + 1) - STEPS_K + CONTEXT_LAG
                    if s == part + (max(due, LAST_SUM_STEP + 1) if due > N_STEP else due):
                        context(q // N_QT, q % N_QT, part)
